import numpy as np
import ml_dtypes


def mxq(x, axis, fmt="e4m3"):
    dtype, down = {"e4m3": (ml_dtypes.float8_e4m3fn, 7), "e5m2": (ml_dtypes.float8_e5m2, 14)}[fmt]
    v = np.moveaxis(np.asarray(x, np.float32).astype(ml_dtypes.bfloat16).astype(np.float64), axis, -1)
    blocks = v.reshape(v.shape[:-1] + (-1, 32))
    amax = np.abs(blocks).max(-1, keepdims=True)
    byte = np.maximum(np.where(amax > 0, np.frexp(amax)[1] - 1 + 127, 0) - down, 1)
    scale = np.exp2(byte - 127.0)
    codes = (blocks / scale).astype(np.float32).astype(dtype).astype(np.float64)
    return np.moveaxis((codes * scale).reshape(v.shape), -1, axis)


WIDE = False


def mx_kscale(k):
    if not WIDE:
        return np.ones(k)
    levels = np.array([10, -10, 5, -5, 0])
    if k % 512:
        return np.exp2(np.random.permutation(np.resize(levels, k // 32))).repeat(32)
    a = np.empty((k // 512, 16))
    for p in range(k // 512):
        a[p, :8] = np.random.permutation(np.resize(levels, 8))
        for g in range(8):
            far = levels[np.abs(levels - a[p, g]) >= 10]
            a[p, g + 8] = far[np.random.randint(len(far))]
    return np.exp2(a.ravel()).repeat(32)


BF16 = ml_dtypes.bfloat16


def bf(x):
    return np.asarray(x, np.float32).astype(BF16)


def f64(x):
    return np.asarray(x).astype(np.float64)


B, T, C, CO, HS, DW, DA, DV, DG = 4, 1024, 1024, 256, 64, 128, 128, 128, 128
H = C // HS
EPS_GN = 0.00064


def setup_inputs():
    n = np.random.standard_normal
    t = mx_kscale(C)
    return {
        "y": bf(n((B, T, C)) * 0.1),
        "r": bf(n((B, T, C))),
        "k": bf(n((B, T, C)) * 0.6),
        "v": bf(n((B, T, C)) * 0.8),
        "g_hid": bf(1.0 / (1.0 + np.exp(-n((B, T, DG))))),
        "g2": bf(n((DG, C)) * 2.0 / np.sqrt(DG) * t),
        "r_k": bf(n((H, HS)) * 0.2 - 0.04),
        "ln_g": bf(1.0 + n((C,)) * 0.1),
        "ln_b": bf(n((C,)) * 0.1),
        "W_o": bf(n((CO, C)) * 0.7 / np.sqrt(C) / t),
    }


def reference(y, r, k, v, g_hid, g2, r_k, ln_g, ln_b, W_o):
    yh = f64(y).reshape(B, T, H, HS)
    mu = np.mean(yh, axis=-1, keepdims=True)
    var = np.mean((yh - mu) ** 2, axis=-1, keepdims=True)
    yn = ((yh - mu) / np.sqrt(var + EPS_GN)).reshape(B, T, C)
    yn = yn * f64(ln_g) + f64(ln_b)
    rh = f64(r).reshape(B, T, H, HS)
    kh = f64(k).reshape(B, T, H, HS)
    vh = f64(v).reshape(B, T, H, HS)
    dot = np.sum(rh * kh * f64(r_k), axis=-1, keepdims=True)
    y2 = yn + (dot * vh).reshape(B, T, C)
    g = f64(g_hid) @ f64(g2)
    z = y2 * g
    return mxq(z, 2, "e4m3") @ mxq(f64(W_o), 1, "e4m3").T

@@ -1,0 +1,345 @@
+from contextlib import ExitStack
+
+import concourse.mybir as mybir
+from concourse.masks import make_identity
+
+F32 = mybir.dt.float32
+BF16 = mybir.dt.bfloat16
+U32 = mybir.dt.uint32
+U8 = mybir.dt.uint8
+FP8X4 = mybir.dt.float8_e4m3fn_x4
+ALU = mybir.AluOpType
+ACTF = mybir.ActivationFunctionType
+AX = mybir.AxisListType
+
+P = 128
+TOK = 4096
+NT = TOK // P
+C = 1024
+CO = 256
+HS = 64
+H = C // HS
+DG = 128
+EPS_GN = 0.00064
+NPASS = C // 512
+JMAX = 4
+M_BATCHES = (1, 1, 2) + (4,) * 7
+Q_BATCHES = (4,) * 7 + (2, 1, 1)
+LD_Y, L_ST = 9, 6
+LD_RK, L_PQ, L_RD = 5, 3, 2
+LD_V = 3
+LD_GH, L_GH = 4, 2
+
+FLOPS = 2 * TOK * DG * C + 2 * TOK * C * CO
+
+
+def batch_maps(sizes):
+    first = []
+    where = {}
+    t = 0
+    for b, n in enumerate(sizes):
+        first.append(t)
+        for j in range(n):
+            where[t + j] = (b, j)
+        t += n
+    return first, where
+
+
+def tile_full_tmix_params_pc_t_kernel(tc, y, r, k, v, g_hid, g2, r_k, ln_g, ln_b, W_o, out):
+    nc = tc.nc
+    y_f = y.flatten_outer_dims()
+    r_f = r.flatten_outer_dims()
+    k_f = k.flatten_outer_dims()
+    v_f = v.flatten_outer_dims()
+    gh_f = g_hid.flatten_outer_dims()
+    out_f = out.flatten_outer_dims()
+    m_first, m_where = batch_maps(M_BATCHES)
+    q_first, q_where = batch_maps(Q_BATCHES)
+
+    with ExitStack() as ctx:
+        const = ctx.enter_context(tc.tile_pool(name="const", bufs=1))
+        ypool = ctx.enter_context(tc.tile_pool(name="ypool", bufs=LD_Y + 2))
+        rkpool = ctx.enter_context(tc.tile_pool(name="rkpool", bufs=LD_RK + 1))
+        vpool = ctx.enter_context(tc.tile_pool(name="vpool", bufs=LD_V + 2))
+        work = ctx.enter_context(tc.tile_pool(name="work", bufs=3))
+        big = ctx.enter_context(tc.tile_pool(name="big", bufs=2))
+        stats = ctx.enter_context(tc.tile_pool(name="stats", bufs=5))
+        small = ctx.enter_context(tc.tile_pool(name="small", bufs=3))
+        psum = ctx.enter_context(tc.psum_pool(name="psum", bufs=2))
+
+        y_of, r_of, k_of, v_of, gh_of, ght_of, q_of, dot_of = {}, {}, {}, {}, {}, {}, {}, {}
+        st_of, rstd_of, shift_of, grp_of = {}, {}, {}, {}
+
+        def ld_y(t):
+            y_t = ypool.tile([P, C], BF16)
+            nc.sync.dma_start(out=y_t[:], in_=y_f[t * P : (t + 1) * P, :])
+            y_of[t] = y_t
+
+        def ld_rk(t):
+            r_t = rkpool.tile([P, C], BF16)
+            nc.sync.dma_start(out=r_t[:], in_=r_f[t * P : (t + 1) * P, :])
+            r_of[t] = r_t
+            k_t = rkpool.tile([P, C], BF16)
+            nc.sync.dma_start(out=k_t[:], in_=k_f[t * P : (t + 1) * P, :])
+            k_of[t] = k_t
+
+        def ld_v(t):
+            v_t = vpool.tile([P, C], BF16)
+            nc.sync.dma_start(out=v_t[:], in_=v_f[t * P : (t + 1) * P, :])
+            v_of[t] = v_t
+
+        def ld_gh(grp_i):
+            gh = small.tile([P, JMAX, DG], BF16)
+            nc.sync.dma_start(
+                out=gh[:],
+                in_=gh_f[grp_i * JMAX * P : (grp_i + 1) * JMAX * P, :].rearrange("(j p) d -> p j d", p=P),
+            )
+            gh_of[grp_i] = gh
+
+        rk_b = const.tile([P, C], BF16)
+        nc.scalar.dma_start(out=rk_b[:], in_=r_k.rearrange("h c -> (h c)").partition_broadcast(P))
+        lng_raw = const.tile([P, NPASS, 4], BF16)
+        nc.scalar.dma_start(out=lng_raw[:], in_=ln_g.rearrange("(g p u) -> p g u", g=NPASS, u=4))
+        lnb_raw = const.tile([P, NPASS, 4], BF16)
+        nc.scalar.dma_start(out=lnb_raw[:], in_=ln_b.rearrange("(g p u) -> p g u", g=NPASS, u=4))
+        g2_sb = const.tile([P, C], BF16)
+        w_raw = const.tile([P, 2, C], BF16)
+
+        ld_rk(0)
+        ld_y(0)
+        ld_y(1)
+        ld_y(2)
+        ld_rk(1)
+        ld_y(3)
+        ld_y(4)
+        ld_v(0)
+        ld_y(5)
+        ld_gh(0)
+        nc.sync.dma_start(out=g2_sb[:], in_=g2)
+        ld_y(6)
+        ld_rk(2)
+        ld_y(7)
+        ld_y(8)
+        ld_v(1)
+        nc.sync.dma_start(out=w_raw[:], in_=W_o.rearrange("(a p) c -> p a c", p=P))
+        ld_rk(3)
+        ld_v(2)
+        ld_rk(4)
+
+        ident_b = const.tile([P, P], BF16)
+        make_identity(nc, ident_b[:])
+        ident_f = const.tile([P, P], F32)
+        make_identity(nc, ident_f[:])
+        zero_t = const.tile([P, 1], F32)
+        nc.gpsimd.memset(zero_t[:], 0.0)
+        eps_t = const.tile([P, 1], F32)
+        nc.vector.tensor_scalar(
+            out=eps_t[:], in0=zero_t[:], scalar1=1.0, scalar2=EPS_GN, op0=ALU.mult, op1=ALU.add
+        )
+
+        lgb = const.tile([P, 16], F32)
+        nc.vector.tensor_copy(out=lgb[:, 0:8], in_=lng_raw[:].rearrange("p g u -> p (g u)"))
+        nc.vector.tensor_copy(out=lgb[:, 8:16], in_=lnb_raw[:].rearrange("p g u -> p (g u)"))
+        g2_perm = const.tile([P, C], BF16)
+        nc.scalar.copy(
+            out=g2_perm[:].rearrange("k (g u p) -> k g u p", g=NPASS, u=4),
+            in_=g2_sb[:].rearrange("k (g p u) -> k g u p", g=NPASS, u=4),
+        )
+
+        w_codes = const.tile([P, NPASS * CO], U32, align_bytes=64)
+        w_scales = const.tile([P, NPASS * CO], U8, align_bytes=64)
+
+        def prep_w():
+            for g in range(NPASS):
+                w_t = psum.tile([P, 4, CO], BF16, tag="misc", bufs=1)
+                for t in range(4):
+                    for a in range(2):
+                        nc.tensor.transpose(
+                            w_t[:, t, a * P : (a + 1) * P],
+                            w_raw[:, a, g * 512 + t : (g + 1) * 512 : 4],
+                            ident_b[:],
+                        )
+                w_grp = const.tile([P, CO, 4], BF16, align_bytes=64)
+                nc.scalar.copy(out=w_grp[:], in_=w_t[:].rearrange("p t o -> p o t"))
+                nc.vector.quantize_mx(
+                    out=w_codes[:, g * CO : (g + 1) * CO].bitcast(FP8X4),
+                    scales=w_scales[:, g * CO : (g + 1) * CO],
+                    in_=w_grp[:].rearrange("p o t -> p (o t)"),
+                )
+
+        def pq(t):
+            q = work.tile([P, C], F32)
+            nc.gpsimd.tensor_tensor(out=q[:], in0=r_of[t][:], in1=k_of[t][:], op=ALU.mult)
+            nc.gpsimd.tensor_tensor(out=q[:], in0=q[:], in1=rk_b[:], op=ALU.mult)
+            q_of[t] = q
+
+        def rd(t):
+            dot = stats.tile([P, H], F32, bufs=6)
+            nc.vector.tensor_reduce(
+                out=dot[:], in_=q_of[t][:].rearrange("p (h c) -> p h c", c=HS), axis=AX.X, op=ALU.add
+            )
+            dot_of[t] = dot
+
+        def st_stage(t):
+            b, j = m_where[t]
+            if j == 0:
+                st = stats.tile([P, JMAX * H * 3], F32)
+                st_of[b] = st
+            st = st_of[b]
+            for hp in range(H // 2):
+                i0 = (j * (H // 2) + hp) * 6
+                nc.vector.bn_stats(
+                    out=st[:, i0 : i0 + 6],
+                    in_=y_of[t][:, hp * 2 * HS : (hp + 1) * 2 * HS].rearrange("p (h c) -> p c h", h=2),
+                )
+            if j == M_BATCHES[b] - 1:
+                nh = M_BATCHES[b] * H
+                st_v = st[:].rearrange("p (n t) -> p n t", t=3)
+                std = stats.tile([P, JMAX * H], F32)
+                nc.scalar.activation(
+                    out=std[:, :nh], in_=st_v[:, :nh, 2], func=ACTF.Sqrt, bias=eps_t[:, 0:1], scale=1.0 / HS
+                )
+                negmean = stats.tile([P, JMAX * H], F32)
+                nc.scalar.activation(out=negmean[:, :nh], in_=st_v[:, :nh, 1], func=ACTF.Copy, scale=-1.0)
+                rstd = stats.tile([P, JMAX * H], F32)
+                nc.vector.reciprocal(out=rstd[:, :nh], in_=std[:, :nh])
+                shift = stats.tile([P, JMAX * H], F32)
+                nc.gpsimd.tensor_tensor(
+                    out=shift[:, :nh], in0=negmean[:, :nh], in1=rstd[:, :nh], op=ALU.mult
+                )
+                rstd_of[b] = rstd
+                shift_of[b] = shift
+
+        def gh_stage(grp_i):
+            gh_ps = psum.tile([P, JMAX, P], BF16, tag="misc", bufs=1)
+            for j in range(JMAX):
+                nc.tensor.transpose(gh_ps[:, j, :], gh_of[grp_i][:, j, :], ident_b[:])
+            gh_t = small.tile([P, JMAX, P], BF16)
+            nc.scalar.copy(out=gh_t[:], in_=gh_ps[:])
+            ght_of[grp_i] = gh_t
+
+        def late(t):
+            mb, mj = m_where[t]
+            qb, qj = q_where[t]
+            rstd, shift, dot = rstd_of[mb], shift_of[mb], dot_of[t]
+            y_t, v_t = y_of[t], v_of[t]
+            if qj == 0:
+                grp = big.tile([P, JMAX, NPASS, P, 4], BF16, align_bytes=64)
+                grp_of[qb] = grp
+            grp = grp_of[qb]
+            n_t = work.tile([P, C], F32)
+            w_t2 = work.tile([P, C], F32)
+            n_v = n_t[:].rearrange("p (g u q) -> p g u q", g=NPASS, u=4)
+            w_v = w_t2[:].rearrange("p (g u q) -> p g u q", g=NPASS, u=4)
+            for h in range(H):
+                col = mj * H + h
+                cs = slice(h * HS, (h + 1) * HS)
+                hq = slice((h % 8) * 16, (h % 8) * 16 + 16)
+                nc.scalar.activation(
+                    out=n_v[:, h // 8, :, hq],
+                    in_=y_t[:, cs].rearrange("p (q u) -> p u q", u=4),
+                    func=ACTF.Identity,
+                    bias=shift[:, col : col + 1],
+                    scale=rstd[:, col : col + 1],
+                )
+                nc.scalar.activation(
+                    out=w_v[:, h // 8, :, hq],
+                    in_=v_t[:, cs].rearrange("p (q u) -> p u q", u=4),
+                    func=ACTF.Copy,
+                    scale=dot[:, h : h + 1],
+                )
+            for g in range(NPASS):
+                n_ps = psum.tile([P, 4, P], F32)
+                w_ps = psum.tile([P, 4, P], F32)
+                g_ps = psum.tile([P, 4, P], F32)
+                for u in range(4):
+                    cb = g * 4 + u
+                    nc.tensor.transpose(n_ps[:, u, :], n_t[:, cb * P : (cb + 1) * P], ident_f[:])
+                for u in range(4):
+                    cb = g * 4 + u
+                    nc.tensor.transpose(w_ps[:, u, :], w_t2[:, cb * P : (cb + 1) * P], ident_f[:])
+                for u in range(4):
+                    cb = g * 4 + u
+                    nc.tensor.matmul(
+                        g_ps[:, u, :],
+                        lhsT=g2_perm[:, cb * P : (cb + 1) * P],
+                        rhs=ght_of[t // JMAX][:, t % JMAX, :],
+                        start=True,
+                        stop=True,
+                    )
+                e_t = work.tile([P, 4, P], F32)
+                for u in range(4):
+                    cb = g * 4 + u
+                    nc.scalar.activation(
+                        out=e_t[:, u, :],
+                        in_=n_ps[:, u, :],
+                        func=ACTF.Identity,
+                        bias=lgb[:, 8 + cb : 9 + cb],
+                        scale=lgb[:, cb : cb + 1],
+                    )
+                f_t = work.tile([P, 4, P], F32)
+                nc.vector.tensor_tensor(out=f_t[:], in0=e_t[:], in1=w_ps[:], op=ALU.add)
+                nc.vector.tensor_tensor(
+                    out=grp[:, qj, g],
+                    in0=f_t[:].rearrange("p u m -> p m u"),
+                    in1=g_ps[:].rearrange("p u m -> p m u"),
+                    op=ALU.mult,
+                )
+            if qj == Q_BATCHES[qb] - 1:
+                finish(qb)
+
+        def finish(qb):
+            nb = Q_BATCHES[qb]
+            grp = grp_of[qb]
+            z_codes = big.tile([P, JMAX * NPASS * P], U32, align_bytes=64)
+            z_scales = big.tile([P, JMAX * NPASS * P], U8, align_bytes=64)
+            nw = nb * NPASS * P
+            nc.vector.quantize_mx(
+                out=z_codes[:, :nw].bitcast(FP8X4),
+                scales=z_scales[:, :nw],
+                in_=grp[:, :nb].rearrange("p j g m u -> p (j g m u)"),
+            )
+            o_sb = big.tile([P, JMAX, CO], F32)
+            for j0 in range(0, nb, 2):
+                npair = min(2, nb - j0)
+                o_ps = psum.tile([P, 2, CO], F32, bufs=1)
+                for u in range(npair):
+                    for g in range(NPASS):
+                        i0 = ((j0 + u) * NPASS + g) * P
+                        nc.tensor.matmul_mx(
+                            out=o_ps[:, u, :],
+                            lhsT=z_codes[:, i0 : i0 + P].bitcast(FP8X4),
+                            lhsT_scale=z_scales[:, i0 : i0 + P],
+                            rhs=w_codes[:, g * CO : (g + 1) * CO].bitcast(FP8X4),
+                            rhs_scale=w_scales[:, g * CO : (g + 1) * CO],
+                            start=(g == 0),
+                            stop=(g == NPASS - 1),
+                        )
+                nc.scalar.copy(out=o_sb[:, j0 : j0 + npair, :], in_=o_ps[:, :npair, :])
+            t0 = q_first[qb] * P
+            nc.scalar.dma_start(
+                out=out_f[t0 : t0 + nb * P, :].rearrange("(j p) o -> p j o", p=P), in_=o_sb[:, :nb, :]
+            )
+
+        for i in range(-L_ST, NT):
+            if i >= 0:
+                if i + LD_Y < NT:
+                    ld_y(i + LD_Y)
+                if i + LD_RK < NT:
+                    ld_rk(i + LD_RK)
+                if i + LD_V < NT:
+                    ld_v(i + LD_V)
+                if (i + LD_GH) % JMAX == 0 and i + LD_GH < NT:
+                    ld_gh((i + LD_GH) // JMAX)
+            if 0 <= i + L_PQ < NT:
+                pq(i + L_PQ)
+            if 0 <= i + L_ST < NT:
+                st_stage(i + L_ST)
+            if 0 <= i + L_RD < NT:
+                rd(i + L_RD)
+            if (i + L_GH) % JMAX == 0 and 0 <= i + L_GH < NT:
+                gh_stage((i + L_GH) // JMAX)
+            if i == -1:
+                prep_w()
+            if i >= 0:
+                late(i)

@@ -23,12 +23,13 @@ DG = 128
 EPS_GN = 0.00064
 NPASS = C // 512
 JMAX = 4
-M_BATCHES = (1, 1, 2) + (4,) * 7
+DI = 8
+DJ = C // P
+M_BATCHES = (1, 2, 2, 2) + (4,) * 6 + (1,)
 Q_BATCHES = (4,) * 7 + (2, 1, 1)
-LD_Y, L_ST = 9, 6
-LD_RK, L_PQ, L_RD = 5, 3, 2
-LD_V = 3
-LD_GH, L_GH = 4, 2
+LD = 9
+LD_Y = LD + 2
+LD_V = 7
 
 FLOPS = 2 * TOK * DG * C + 2 * TOK * C * CO
 
@@ -58,9 +59,9 @@ def tile_full_tmix_params_pc_t_kernel(tc, y, r, k, v, g_hid, g2, r_k, ln_g, ln_b
 
     with ExitStack() as ctx:
         const = ctx.enter_context(tc.tile_pool(name="const", bufs=1))
-        ypool = ctx.enter_context(tc.tile_pool(name="ypool", bufs=LD_Y + 2))
-        rkpool = ctx.enter_context(tc.tile_pool(name="rkpool", bufs=LD_RK + 1))
-        vpool = ctx.enter_context(tc.tile_pool(name="vpool", bufs=LD_V + 2))
+        ypool = ctx.enter_context(tc.tile_pool(name="ypool", bufs=LD_Y + 1))
+        rkpool = ctx.enter_context(tc.tile_pool(name="rkpool", bufs=LD - 2))
+        vpool = ctx.enter_context(tc.tile_pool(name="vpool", bufs=LD_V + 1))
         work = ctx.enter_context(tc.tile_pool(name="work", bufs=3))
         big = ctx.enter_context(tc.tile_pool(name="big", bufs=2))
         stats = ctx.enter_context(tc.tile_pool(name="stats", bufs=5))
@@ -68,7 +69,8 @@ def tile_full_tmix_params_pc_t_kernel(tc, y, r, k, v, g_hid, g2, r_k, ln_g, ln_b
         psum = ctx.enter_context(tc.psum_pool(name="psum", bufs=2))
 
         y_of, r_of, k_of, v_of, gh_of, ght_of, q_of, dot_of = {}, {}, {}, {}, {}, {}, {}, {}
-        st_of, rstd_of, shift_of, grp_of = {}, {}, {}, {}
+        st_of, std_of, nm_of, rstd_of, shift_of, grp_of, z_of, wg_of, o_of = {}, {}, {}, {}, {}, {}, {}, {}, {}
+        nt_of, wt_of, nps_of, wps_of, gps_of, e_of, f_of, dps_of, dsb_of = {}, {}, {}, {}, {}, {}, {}, {}, {}
 
         def ld_y(t):
             y_t = ypool.tile([P, C], BF16)
@@ -105,27 +107,6 @@ def tile_full_tmix_params_pc_t_kernel(tc, y, r, k, v, g_hid, g2, r_k, ln_g, ln_b
         g2_sb = const.tile([P, C], BF16)
         w_raw = const.tile([P, 2, C], BF16)
 
-        ld_rk(0)
-        ld_y(0)
-        ld_y(1)
-        ld_y(2)
-        ld_rk(1)
-        ld_y(3)
-        ld_y(4)
-        ld_v(0)
-        ld_y(5)
-        ld_gh(0)
-        nc.sync.dma_start(out=g2_sb[:], in_=g2)
-        ld_y(6)
-        ld_rk(2)
-        ld_y(7)
-        ld_y(8)
-        ld_v(1)
-        nc.sync.dma_start(out=w_raw[:], in_=W_o.rearrange("(a p) c -> p a c", p=P))
-        ld_rk(3)
-        ld_v(2)
-        ld_rk(4)
-
         ident_b = const.tile([P, P], BF16)
         make_identity(nc, ident_b[:])
         ident_f = const.tile([P, P], F32)
@@ -136,210 +117,386 @@ def tile_full_tmix_params_pc_t_kernel(tc, y, r, k, v, g_hid, g2, r_k, ln_g, ln_b
         nc.vector.tensor_scalar(
             out=eps_t[:], in0=zero_t[:], scalar1=1.0, scalar2=EPS_GN, op0=ALU.mult, op1=ALU.add
         )
-
         lgb = const.tile([P, 16], F32)
         nc.vector.tensor_copy(out=lgb[:, 0:8], in_=lng_raw[:].rearrange("p g u -> p (g u)"))
         nc.vector.tensor_copy(out=lgb[:, 8:16], in_=lnb_raw[:].rearrange("p g u -> p (g u)"))
-        g2_perm = const.tile([P, C], BF16)
+        rk_perm = const.tile([P, C], BF16)
         nc.scalar.copy(
-            out=g2_perm[:].rearrange("k (g u p) -> k g u p", g=NPASS, u=4),
-            in_=g2_sb[:].rearrange("k (g p u) -> k g u p", g=NPASS, u=4),
+            out=rk_perm[:].rearrange("p (j h i) -> p j h i", j=DJ, i=DI),
+            in_=rk_b[:].rearrange("p (h j i) -> p j h i", j=DJ, i=DI),
         )
-
+        g2_perm = const.tile([P, C], BF16)
         w_codes = const.tile([P, NPASS * CO], U32, align_bytes=64)
         w_scales = const.tile([P, NPASS * CO], U8, align_bytes=64)
 
-        def prep_w():
-            for g in range(NPASS):
-                w_t = psum.tile([P, 4, CO], BF16, tag="misc", bufs=1)
-                for t in range(4):
-                    for a in range(2):
-                        nc.tensor.transpose(
-                            w_t[:, t, a * P : (a + 1) * P],
-                            w_raw[:, a, g * 512 + t : (g + 1) * 512 : 4],
-                            ident_b[:],
-                        )
-                w_grp = const.tile([P, CO, 4], BF16, align_bytes=64)
-                nc.scalar.copy(out=w_grp[:], in_=w_t[:].rearrange("p t o -> p o t"))
-                nc.vector.quantize_mx(
-                    out=w_codes[:, g * CO : (g + 1) * CO].bitcast(FP8X4),
-                    scales=w_scales[:, g * CO : (g + 1) * CO],
-                    in_=w_grp[:].rearrange("p o t -> p (o t)"),
-                )
+        def prep_g2():
+            nc.scalar.copy(
+                out=g2_perm[:].rearrange("k (g u p) -> k g u p", g=NPASS, u=4),
+                in_=g2_sb[:].rearrange("k (g p u) -> k g u p", g=NPASS, u=4),
+            )
 
-        def pq(t):
-            q = work.tile([P, C], F32)
-            nc.gpsimd.tensor_tensor(out=q[:], in0=r_of[t][:], in1=k_of[t][:], op=ALU.mult)
-            nc.gpsimd.tensor_tensor(out=q[:], in0=q[:], in1=rk_b[:], op=ALU.mult)
+        def proj_turn(g):
+            w_t = psum.tile([P, 4, CO], BF16, tag="misc", bufs=1)
+            for t in range(4):
+                for a in range(2):
+                    nc.tensor.transpose(
+                        w_t[:, t, a * P : (a + 1) * P],
+                        w_raw[:, a, g * 512 + t : (g + 1) * 512 : 4],
+                        ident_b[:],
+                    )
+            wg_of[g] = w_t
+
+        def proj_copy(g):
+            w_grp = const.tile([P, CO, 4], BF16, align_bytes=64, bufs=2)
+            nc.scalar.copy(out=w_grp[:], in_=wg_of[g][:].rearrange("p t o -> p o t"))
+            wg_of[g] = w_grp
+
+        def proj_quant(g):
+            nc.vector.quantize_mx(
+                out=w_codes[:, g * CO : (g + 1) * CO].bitcast(FP8X4),
+                scales=w_scales[:, g * CO : (g + 1) * CO],
+                in_=wg_of[g][:].rearrange("p o t -> p (o t)"),
+            )
+
+        def pair_rk(t):
+            eng = nc.vector if t % JMAX == 0 else nc.gpsimd
+            p_t = work.tile([P, C], F32, bufs=3)
+            eng.tensor_tensor(out=p_t[:], in0=r_of[t][:], in1=k_of[t][:], op=ALU.mult)
+            q_of[t] = p_t
+
+        def weigh(t):
+            eng = nc.vector if t == 0 else nc.gpsimd
+            q = work.tile([P, C], F32, bufs=4)
+            eng.tensor_tensor(
+                out=q[:].rearrange("p (j h i) -> p j h i", j=DJ, i=DI),
+                in0=q_of[t][:].rearrange("p (h j i) -> p j h i", j=DJ, i=DI),
+                in1=rk_perm[:].rearrange("p (j h i) -> p j h i", j=DJ, i=DI),
+                op=ALU.mult,
+            )
             q_of[t] = q
 
-        def rd(t):
-            dot = stats.tile([P, H], F32, bufs=6)
+        def dot_fold(t):
+            d_ps = psum.tile([P, 2, P], F32, tag="dot", bufs=1)
+            for j in range(DJ):
+                nc.tensor.matmul(
+                    d_ps[:, 0, :],
+                    lhsT=q_of[t][:, j * P : (j + 1) * P],
+                    rhs=ident_f[:],
+                    is_transpose=True,
+                    start=(j == 0),
+                    stop=(j == DJ - 1),
+                )
+            dps_of[t] = d_ps
+
+        def dot_copy(t):
+            d_sb = small.tile([P, P], F32)
+            nc.vector.tensor_copy(out=d_sb[:], in_=dps_of[t][:, 0, :])
+            dsb_of[t] = d_sb
+
+        def dot_back(t):
+            nc.tensor.transpose(dps_of[t][:, 1, :], dsb_of[t][:], ident_f[:])
+
+        def dot_sum(t):
+            dot = stats.tile([P, H], F32)
             nc.vector.tensor_reduce(
-                out=dot[:], in_=q_of[t][:].rearrange("p (h c) -> p h c", c=HS), axis=AX.X, op=ALU.add
+                out=dot[:],
+                in_=dps_of[t][:, 1, :].rearrange("p (h i) -> p h i", i=DI),
+                axis=AX.X,
+                op=ALU.add,
             )
             dot_of[t] = dot
 
-        def st_stage(t):
+        def bn(t, half):
             b, j = m_where[t]
-            if j == 0:
+            if j == 0 and half == 0:
                 st = stats.tile([P, JMAX * H * 3], F32)
                 st_of[b] = st
             st = st_of[b]
-            for hp in range(H // 2):
+            for hp in range(half * 4, half * 4 + 4):
                 i0 = (j * (H // 2) + hp) * 6
                 nc.vector.bn_stats(
                     out=st[:, i0 : i0 + 6],
                     in_=y_of[t][:, hp * 2 * HS : (hp + 1) * 2 * HS].rearrange("p (h c) -> p c h", h=2),
                 )
-            if j == M_BATCHES[b] - 1:
-                nh = M_BATCHES[b] * H
-                st_v = st[:].rearrange("p (n t) -> p n t", t=3)
-                std = stats.tile([P, JMAX * H], F32)
-                nc.scalar.activation(
-                    out=std[:, :nh], in_=st_v[:, :nh, 2], func=ACTF.Sqrt, bias=eps_t[:, 0:1], scale=1.0 / HS
-                )
-                negmean = stats.tile([P, JMAX * H], F32)
-                nc.scalar.activation(out=negmean[:, :nh], in_=st_v[:, :nh, 1], func=ACTF.Copy, scale=-1.0)
-                rstd = stats.tile([P, JMAX * H], F32)
-                nc.vector.reciprocal(out=rstd[:, :nh], in_=std[:, :nh])
-                shift = stats.tile([P, JMAX * H], F32)
-                nc.gpsimd.tensor_tensor(
-                    out=shift[:, :nh], in0=negmean[:, :nh], in1=rstd[:, :nh], op=ALU.mult
-                )
-                rstd_of[b] = rstd
-                shift_of[b] = shift
 
-        def gh_stage(grp_i):
+        def std_stage(b):
+            nh = M_BATCHES[b] * H
+            st_v = st_of[b][:].rearrange("p (n t) -> p n t", t=3)
+            std = stats.tile([P, JMAX * H], F32)
+            nc.scalar.activation(
+                out=std[:, :nh], in_=st_v[:, :nh, 2], func=ACTF.Sqrt, bias=eps_t[:, 0:1], scale=1.0 / HS
+            )
+            negmean = stats.tile([P, JMAX * H], F32)
+            nc.scalar.activation(out=negmean[:, :nh], in_=st_v[:, :nh, 1], func=ACTF.Copy, scale=-1.0)
+            nm_of[b] = negmean
+            std_of[b] = std
+
+        def rstd_stage(b):
+            nh = M_BATCHES[b] * H
+            rstd = stats.tile([P, JMAX * H], F32)
+            nc.vector.reciprocal(out=rstd[:, :nh], in_=std_of[b][:, :nh])
+            rstd_of[b] = rstd
+
+        def shift_stage(b):
+            nh = M_BATCHES[b] * H
+            shift = stats.tile([P, JMAX * H], F32)
+            nc.gpsimd.tensor_tensor(
+                out=shift[:, :nh], in0=nm_of[b][:, :nh], in1=rstd_of[b][:, :nh], op=ALU.mult
+            )
+            shift_of[b] = shift
+
+        def gh_turn(grp_i):
             gh_ps = psum.tile([P, JMAX, P], BF16, tag="misc", bufs=1)
             for j in range(JMAX):
                 nc.tensor.transpose(gh_ps[:, j, :], gh_of[grp_i][:, j, :], ident_b[:])
+            ght_of[grp_i] = gh_ps
+
+        def gh_copy(grp_i):
             gh_t = small.tile([P, JMAX, P], BF16)
-            nc.scalar.copy(out=gh_t[:], in_=gh_ps[:])
+            nc.scalar.copy(out=gh_t[:], in_=ght_of[grp_i][:])
             ght_of[grp_i] = gh_t
 
-        def late(t):
+        def norm_rows(t):
             mb, mj = m_where[t]
-            qb, qj = q_where[t]
-            rstd, shift, dot = rstd_of[mb], shift_of[mb], dot_of[t]
-            y_t, v_t = y_of[t], v_of[t]
-            if qj == 0:
-                grp = big.tile([P, JMAX, NPASS, P, 4], BF16, align_bytes=64)
-                grp_of[qb] = grp
-            grp = grp_of[qb]
-            n_t = work.tile([P, C], F32)
-            w_t2 = work.tile([P, C], F32)
-            n_v = n_t[:].rearrange("p (g u q) -> p g u q", g=NPASS, u=4)
-            w_v = w_t2[:].rearrange("p (g u q) -> p g u q", g=NPASS, u=4)
+            rstd, shift = rstd_of[mb], shift_of[mb]
+            n_t = work.tile([P, NPASS, 4, P], F32)
             for h in range(H):
                 col = mj * H + h
-                cs = slice(h * HS, (h + 1) * HS)
-                hq = slice((h % 8) * 16, (h % 8) * 16 + 16)
+                q0 = (h % 8) * 16
                 nc.scalar.activation(
-                    out=n_v[:, h // 8, :, hq],
-                    in_=y_t[:, cs].rearrange("p (q u) -> p u q", u=4),
+                    out=n_t[:, h // 8, :, q0 : q0 + 16],
+                    in_=y_of[t][:, h * HS : (h + 1) * HS].rearrange("p (q u) -> p u q", u=4),
                     func=ACTF.Identity,
                     bias=shift[:, col : col + 1],
                     scale=rstd[:, col : col + 1],
                 )
-                nc.scalar.activation(
-                    out=w_v[:, h // 8, :, hq],
-                    in_=v_t[:, cs].rearrange("p (q u) -> p u q", u=4),
-                    func=ACTF.Copy,
-                    scale=dot[:, h : h + 1],
-                )
-            for g in range(NPASS):
-                n_ps = psum.tile([P, 4, P], F32)
-                w_ps = psum.tile([P, 4, P], F32)
-                g_ps = psum.tile([P, 4, P], F32)
-                for u in range(4):
-                    cb = g * 4 + u
-                    nc.tensor.transpose(n_ps[:, u, :], n_t[:, cb * P : (cb + 1) * P], ident_f[:])
-                for u in range(4):
-                    cb = g * 4 + u
-                    nc.tensor.transpose(w_ps[:, u, :], w_t2[:, cb * P : (cb + 1) * P], ident_f[:])
-                for u in range(4):
-                    cb = g * 4 + u
-                    nc.tensor.matmul(
-                        g_ps[:, u, :],
-                        lhsT=g2_perm[:, cb * P : (cb + 1) * P],
-                        rhs=ght_of[t // JMAX][:, t % JMAX, :],
-                        start=True,
-                        stop=True,
-                    )
-                e_t = work.tile([P, 4, P], F32)
-                for u in range(4):
-                    cb = g * 4 + u
-                    nc.scalar.activation(
-                        out=e_t[:, u, :],
-                        in_=n_ps[:, u, :],
-                        func=ACTF.Identity,
-                        bias=lgb[:, 8 + cb : 9 + cb],
-                        scale=lgb[:, cb : cb + 1],
-                    )
-                f_t = work.tile([P, 4, P], F32)
-                nc.vector.tensor_tensor(out=f_t[:], in0=e_t[:], in1=w_ps[:], op=ALU.add)
-                nc.vector.tensor_tensor(
-                    out=grp[:, qj, g],
-                    in0=f_t[:].rearrange("p u m -> p m u"),
-                    in1=g_ps[:].rearrange("p u m -> p m u"),
-                    op=ALU.mult,
-                )
-            if qj == Q_BATCHES[qb] - 1:
-                finish(qb)
+            nt_of[t] = n_t
 
-        def finish(qb):
+        def bonus_rows(t):
+            w_t2 = work.tile([P, NPASS, 4, P], F32)
+            for h in range(H):
+                q0 = (h % 8) * 16
+                nc.scalar.activation(
+                    out=w_t2[:, h // 8, :, q0 : q0 + 16],
+                    in_=v_of[t][:, h * HS : (h + 1) * HS].rearrange("p (q u) -> p u q", u=4),
+                    func=ACTF.Copy,
+                    scale=dot_of[t][:, h : h + 1],
+                )
+            wt_of[t] = w_t2
+
+        def turn_n(t, g):
+            n_ps = psum.tile([P, 4, P], F32)
+            for u in range(4):
+                nc.tensor.transpose(n_ps[:, u, :], nt_of[t][:, g, u, :], ident_f[:])
+            nps_of[t, g] = n_ps
+
+        def turn_w(t, g):
+            w_ps = psum.tile([P, 4, P], F32)
+            for u in range(4):
+                nc.tensor.transpose(w_ps[:, u, :], wt_of[t][:, g, u, :], ident_f[:])
+            wps_of[t, g] = w_ps
+
+        def gate_mm(t, g):
+            g_ps = psum.tile([P, 4, P], F32)
+            for u in range(4):
+                cb = g * 4 + u
+                nc.tensor.matmul(
+                    g_ps[:, u, :],
+                    lhsT=g2_perm[:, cb * P : (cb + 1) * P],
+                    rhs=ght_of[t // JMAX][:, t % JMAX, :],
+                    start=True,
+                    stop=True,
+                )
+            gps_of[t, g] = g_ps
+
+        def affine(t, g):
+            e_t = work.tile([P, 4, P], F32)
+            for u in range(4):
+                cb = g * 4 + u
+                nc.scalar.activation(
+                    out=e_t[:, u, :],
+                    in_=nps_of[t, g][:, u, :],
+                    func=ACTF.Identity,
+                    bias=lgb[:, 8 + cb : 9 + cb],
+                    scale=lgb[:, cb : cb + 1],
+                )
+            e_of[t, g] = e_t
+
+        def add(t, g):
+            f_t = work.tile([P, 4, P], F32)
+            nc.vector.tensor_tensor(out=f_t[:], in0=e_of[t, g][:], in1=wps_of[t, g][:], op=ALU.add)
+            f_of[t, g] = f_t
+
+        def gate(t, g):
+            qb, qj = q_where[t]
+            if qj == 0 and g == 0:
+                grp = big.tile([P, JMAX, NPASS, P, 4], BF16, align_bytes=64)
+                grp_of[qb] = grp
+            nc.vector.tensor_tensor(
+                out=grp_of[qb][:, qj, g],
+                in0=f_of[t, g][:].rearrange("p u m -> p m u"),
+                in1=gps_of[t, g][:].rearrange("p u m -> p m u"),
+                op=ALU.mult,
+            )
+
+        def quant(qb):
             nb = Q_BATCHES[qb]
-            grp = grp_of[qb]
             z_codes = big.tile([P, JMAX * NPASS * P], U32, align_bytes=64)
             z_scales = big.tile([P, JMAX * NPASS * P], U8, align_bytes=64)
             nw = nb * NPASS * P
             nc.vector.quantize_mx(
                 out=z_codes[:, :nw].bitcast(FP8X4),
                 scales=z_scales[:, :nw],
-                in_=grp[:, :nb].rearrange("p j g m u -> p (j g m u)"),
+                in_=grp_of[qb][:, :nb].rearrange("p j g m u -> p (j g m u)"),
             )
             o_sb = big.tile([P, JMAX, CO], F32)
-            for j0 in range(0, nb, 2):
-                npair = min(2, nb - j0)
-                o_ps = psum.tile([P, 2, CO], F32, bufs=1)
-                for u in range(npair):
-                    for g in range(NPASS):
-                        i0 = ((j0 + u) * NPASS + g) * P
-                        nc.tensor.matmul_mx(
-                            out=o_ps[:, u, :],
-                            lhsT=z_codes[:, i0 : i0 + P].bitcast(FP8X4),
-                            lhsT_scale=z_scales[:, i0 : i0 + P],
-                            rhs=w_codes[:, g * CO : (g + 1) * CO].bitcast(FP8X4),
-                            rhs_scale=w_scales[:, g * CO : (g + 1) * CO],
-                            start=(g == 0),
-                            stop=(g == NPASS - 1),
-                        )
-                nc.scalar.copy(out=o_sb[:, j0 : j0 + npair, :], in_=o_ps[:, :npair, :])
+            z_of[qb] = (z_codes, z_scales, o_sb)
+
+        def project(qb, j0):
+            z_codes, z_scales, o_sb = z_of[qb]
+            npair = min(2, Q_BATCHES[qb] - j0)
+            o_ps = psum.tile([P, 2, CO], F32, tag="misc", bufs=1)
+            for u in range(npair):
+                for g in range(NPASS):
+                    i0 = ((j0 + u) * NPASS + g) * P
+                    nc.tensor.matmul_mx(
+                        out=o_ps[:, u, :],
+                        lhsT=z_codes[:, i0 : i0 + P].bitcast(FP8X4),
+                        lhsT_scale=z_scales[:, i0 : i0 + P],
+                        rhs=w_codes[:, g * CO : (g + 1) * CO].bitcast(FP8X4),
+                        rhs_scale=w_scales[:, g * CO : (g + 1) * CO],
+                        start=(g == 0),
+                        stop=(g == NPASS - 1),
+                    )
+            o_of[qb, j0] = o_ps
+
+        def collect(qb, j0):
+            npair = min(2, Q_BATCHES[qb] - j0)
+            o_ps = o_of[qb, j0]
+            nc.vector.tensor_copy(out=z_of[qb][2][:, j0 : j0 + npair, :], in_=o_ps[:, :npair, :])
+
+        def store(qb):
             t0 = q_first[qb] * P
-            nc.scalar.dma_start(
-                out=out_f[t0 : t0 + nb * P, :].rearrange("(j p) o -> p j o", p=P), in_=o_sb[:, :nb, :]
+            nb = Q_BATCHES[qb]
+            nc.sync.dma_start(
+                out=out_f[t0 : t0 + nb * P, :].rearrange("(j p) o -> p j o", p=P), in_=z_of[qb][2][:, :nb, :]
             )
 
-        for i in range(-L_ST, NT):
-            if i >= 0:
-                if i + LD_Y < NT:
-                    ld_y(i + LD_Y)
-                if i + LD_RK < NT:
-                    ld_rk(i + LD_RK)
-                if i + LD_V < NT:
-                    ld_v(i + LD_V)
-                if (i + LD_GH) % JMAX == 0 and i + LD_GH < NT:
-                    ld_gh((i + LD_GH) // JMAX)
-            if 0 <= i + L_PQ < NT:
-                pq(i + L_PQ)
-            if 0 <= i + L_ST < NT:
-                st_stage(i + L_ST)
-            if 0 <= i + L_RD < NT:
-                rd(i + L_RD)
-            if (i + L_GH) % JMAX == 0 and 0 <= i + L_GH < NT:
-                gh_stage((i + L_GH) // JMAX)
-            if i == -1:
-                prep_w()
-            if i >= 0:
-                late(i)
+        rec_due = {-3: 0, -1: 1, 0: 2, 2: 3}
+        for b in range(4, len(M_BATCHES)):
+            rec_due[m_first[b] - 3] = b
+        shift_due = {-2: 0, -1: 1, 1: 2, 2: 3}
+        for b in range(4, len(M_BATCHES)):
+            shift_due[m_first[b] - 3] = b
+        bn_due = {-3: [0], -2: [1], -1: [2, 3], 0: [4, 5], 1: [6, 7], 2: [8, 9], 3: [10]}
+        for t in range(11, NT):
+            bn_due[t - 7] = [t]
+        fin_due = {q_first[b] + Q_BATCHES[b]: b for b in range(len(Q_BATCHES))}
+        y_next = 0
+
+        ctx.enter_context(tc.manual_schedule())
+        for i in range(-LD, NT + 4):
+            s = i + LD
+            if 0 <= s < NT:
+                ld_rk(s)
+            while y_next < min(NT, s + min(s, 3) + 1):
+                ld_y(y_next)
+                y_next += 1
+            if 0 <= i + LD_V < NT:
+                ld_v(i + LD_V)
+            if s % JMAX == 2 and s // JMAX < NT // JMAX:
+                ld_gh(s // JMAX)
+            if s == 1:
+                nc.sync.dma_start(out=g2_sb[:], in_=g2)
+            if i == -3:
+                nc.sync.dma_start(out=w_raw[:], in_=W_o.rearrange("(a p) c -> p a c", p=P))
+            live = 0 <= i < NT
+            prev = 0 <= i - 1 < NT
+            nxt = 0 <= i + 1 < NT
+            fold = 0 <= i + 2 < NT
+            prod = 0 <= i + 3 < NT
+            bl = bn_due.get(i, [])
+            if i == -3:
+                pair_rk(0)
+                weigh(0)
+            if nxt:
+                norm_rows(i + 1)
+            if live:
+                turn_n(i, 0)
+                turn_w(i, 0)
+            if prev:
+                gate(i - 1, 1)
+            if live:
+                gate_mm(i, 0)
+                affine(i, 0)
+            for t in bl[:1]:
+                bn(t, 0)
+                if i < 4:
+                    bn(t, 1)
+            if fold:
+                dot_fold(i + 2)
+            if (i + 1) % JMAX == 0 and 0 <= i + 1 < NT:
+                gh_turn((i + 1) // JMAX)
+            if live:
+                add(i, 0)
+            if i in rec_due:
+                std_stage(rec_due[i])
+            if nxt:
+                bonus_rows(i + 1)
+            if i - 1 in fin_due:
+                project(fin_due[i - 1], 0)
+            if i - 2 in fin_due and Q_BATCHES[fin_due[i - 2]] > 2:
+                project(fin_due[i - 2], 2)
+            if live:
+                turn_n(i, 1)
+                turn_w(i, 1)
+                affine(i, 1)
+            if (i + 1) % JMAX == 0 and 0 <= i + 1 < NT:
+                gh_copy((i + 1) // JMAX)
+            if fold:
+                dot_copy(i + 2)
+                dot_back(i + 2)
+            if live:
+                gate_mm(i, 1)
+            if i >= 4:
+                for t in bl:
+                    bn(t, 1)
+            else:
+                for t in bl[1:]:
+                    bn(t, 0)
+                    bn(t, 1)
+            if live:
+                gate(i, 0)
+            if fold:
+                dot_sum(i + 2)
+            if i in fin_due:
+                quant(fin_due[i])
+            if i >= 0 and (i + 4) % JMAX == 0 and i + 4 < NT:
+                pair_rk(i + 4)
+            if i in rec_due:
+                rstd_stage(rec_due[i])
+            if prod and i > -3 and (i + 3) % JMAX != 0:
+                pair_rk(i + 3)
+            if i in shift_due and i < 4:
+                shift_stage(shift_due[i])
+            if prod and i > -3:
+                weigh(i + 3)
+            if i in shift_due and i >= 4:
+                shift_stage(shift_due[i])
+            if i - 1 in fin_due:
+                collect(fin_due[i - 1], 0)
+            if i - 2 in fin_due and Q_BATCHES[fin_due[i - 2]] > 2:
+                collect(fin_due[i - 2], 2)
+            if live:
+                add(i, 1)
+            if i == -3:
+                prep_g2()
+            if i in (1, 2):
+                proj_turn(i - 1)
+                proj_copy(i - 1)
+            if i in (2, 3):
+                proj_quant(i - 2)
+            if i - 2 in fin_due and Q_BATCHES[fin_due[i - 2]] <= 2:
+                store(fin_due[i - 2])
+            if i - 3 in fin_due and Q_BATCHES[fin_due[i - 3]] > 2:
+                store(fin_due[i - 3])

@@ -333,9 +333,9 @@ def tile_full_tmix_params_pc_t_kernel(tc, y, r, k, v, g_hid, g2, r_k, ln_g, ln_b
                 grp = big.tile([P, JMAX, NPASS, P, 4], BF16, align_bytes=64)
                 grp_of[qb] = grp
             nc.vector.tensor_tensor(
-                out=grp_of[qb][:, qj, g],
-                in0=f_of[t, g][:].rearrange("p u m -> p m u"),
-                in1=gps_of[t, g][:].rearrange("p u m -> p m u"),
+                out=grp_of[qb][:, qj, g].rearrange("p (c i) u -> p c u i", i=4),
+                in0=f_of[t, g][:].rearrange("p u (c i) -> p c u i", i=4),
+                in1=gps_of[t, g][:].rearrange("p u (c i) -> p c u i", i=4),
                 op=ALU.mult,
             )
 

@@ -25,7 +25,7 @@ NPASS = C // 512
 JMAX = 4
 DI = 8
 DJ = C // P
-M_BATCHES = (1, 2, 2, 2) + (4,) * 6 + (1,)
+M_BATCHES = (1, 1, 1, 2, 2) + (4,) * 6 + (1,)
 Q_BATCHES = (4,) * 7 + (2, 1, 1)
 LD = 9
 LD_Y = LD + 2
@@ -69,7 +69,7 @@ def tile_full_tmix_params_pc_t_kernel(tc, y, r, k, v, g_hid, g2, r_k, ln_g, ln_b
         psum = ctx.enter_context(tc.psum_pool(name="psum", bufs=2))
 
         y_of, r_of, k_of, v_of, gh_of, ght_of, q_of, dot_of = {}, {}, {}, {}, {}, {}, {}, {}
-        st_of, std_of, nm_of, rstd_of, shift_of, grp_of, z_of, wg_of, o_of = {}, {}, {}, {}, {}, {}, {}, {}, {}
+        st_of, nm_of, rstd_of, shift_of, grp_of, z_of, wg_of, o_of = {}, {}, {}, {}, {}, {}, {}, {}
         nt_of, wt_of, nps_of, wps_of, gps_of, e_of, f_of, dps_of, dsb_of = {}, {}, {}, {}, {}, {}, {}, {}, {}
 
         def ld_y(t):
@@ -98,8 +98,11 @@ def tile_full_tmix_params_pc_t_kernel(tc, y, r, k, v, g_hid, g2, r_k, ln_g, ln_b
             )
             gh_of[grp_i] = gh
 
-        rk_b = const.tile([P, C], BF16)
-        nc.scalar.dma_start(out=rk_b[:], in_=r_k.rearrange("h c -> (h c)").partition_broadcast(P))
+        rk_row = const.tile([P, C], BF16)
+        nc.vector.memset(rk_row[:], 0.0)
+        nc.scalar.dma_start(out=rk_row[0:1, :], in_=r_k.rearrange("(o h) c -> o (h c)", o=1))
+        ones_b = const.tile([P, P], BF16)
+        nc.gpsimd.memset(ones_b[:], 1.0)
         lng_raw = const.tile([P, NPASS, 4], BF16)
         nc.scalar.dma_start(out=lng_raw[:], in_=ln_g.rearrange("(g p u) -> p g u", g=NPASS, u=4))
         lnb_raw = const.tile([P, NPASS, 4], BF16)
@@ -118,13 +121,22 @@ def tile_full_tmix_params_pc_t_kernel(tc, y, r, k, v, g_hid, g2, r_k, ln_g, ln_b
             out=eps_t[:], in0=zero_t[:], scalar1=1.0, scalar2=EPS_GN, op0=ALU.mult, op1=ALU.add
         )
         lgb = const.tile([P, 16], F32)
-        nc.vector.tensor_copy(out=lgb[:, 0:8], in_=lng_raw[:].rearrange("p g u -> p (g u)"))
-        nc.vector.tensor_copy(out=lgb[:, 8:16], in_=lnb_raw[:].rearrange("p g u -> p (g u)"))
-        rk_perm = const.tile([P, C], BF16)
-        nc.scalar.copy(
-            out=rk_perm[:].rearrange("p (j h i) -> p j h i", j=DJ, i=DI),
-            in_=rk_b[:].rearrange("p (h j i) -> p j h i", j=DJ, i=DI),
-        )
+        rk_perm = const.tile([P, DJ, H, DI], BF16)
+
+        def prep_rk():
+            for g in range(NPASS):
+                rk_ps = psum.tile([P, 512], F32, tag=("misc", "dot")[g], bufs=1)
+                nc.tensor.matmul(
+                    rk_ps[:], lhsT=ones_b[:], rhs=rk_row[:, g * 512 : (g + 1) * 512], start=True, stop=True
+                )
+                nc.scalar.copy(
+                    out=rk_perm[:, :, g * 8 : (g + 1) * 8, :],
+                    in_=rk_ps[:].rearrange("p (h j i) -> p j h i", j=DJ, i=DI),
+                )
+
+        def prep_ln():
+            nc.vector.tensor_copy(out=lgb[:, 0:8], in_=lng_raw[:].rearrange("p g u -> p (g u)"))
+            nc.vector.tensor_copy(out=lgb[:, 8:16], in_=lnb_raw[:].rearrange("p g u -> p (g u)"))
         g2_perm = const.tile([P, C], BF16)
         w_codes = const.tile([P, NPASS * CO], U32, align_bytes=64)
         w_scales = const.tile([P, NPASS * CO], U8, align_bytes=64)
@@ -158,19 +170,17 @@ def tile_full_tmix_params_pc_t_kernel(tc, y, r, k, v, g_hid, g2, r_k, ln_g, ln_b
                 in_=wg_of[g][:].rearrange("p o t -> p (o t)"),
             )
 
-        def pair_rk(t):
-            eng = nc.vector if t % JMAX == 0 else nc.gpsimd
+        def pair_rk(eng, t):
             p_t = work.tile([P, C], F32, bufs=3)
             eng.tensor_tensor(out=p_t[:], in0=r_of[t][:], in1=k_of[t][:], op=ALU.mult)
             q_of[t] = p_t
 
-        def weigh(t):
-            eng = nc.vector if t == 0 else nc.gpsimd
-            q = work.tile([P, C], F32, bufs=4)
+        def weigh(eng, t):
+            q = work.tile([P, DJ, H, DI], F32, bufs=4)
             eng.tensor_tensor(
-                out=q[:].rearrange("p (j h i) -> p j h i", j=DJ, i=DI),
+                out=q[:],
                 in0=q_of[t][:].rearrange("p (h j i) -> p j h i", j=DJ, i=DI),
-                in1=rk_perm[:].rearrange("p (j h i) -> p j h i", j=DJ, i=DI),
+                in1=rk_perm[:],
                 op=ALU.mult,
             )
             q_of[t] = q
@@ -180,7 +190,7 @@ def tile_full_tmix_params_pc_t_kernel(tc, y, r, k, v, g_hid, g2, r_k, ln_g, ln_b
             for j in range(DJ):
                 nc.tensor.matmul(
                     d_ps[:, 0, :],
-                    lhsT=q_of[t][:, j * P : (j + 1) * P],
+                    lhsT=q_of[t][:, j].rearrange("p h i -> p (h i)"),
                     rhs=ident_f[:],
                     is_transpose=True,
                     start=(j == 0),
@@ -219,22 +229,20 @@ def tile_full_tmix_params_pc_t_kernel(tc, y, r, k, v, g_hid, g2, r_k, ln_g, ln_b
                     in_=y_of[t][:, hp * 2 * HS : (hp + 1) * 2 * HS].rearrange("p (h c) -> p c h", h=2),
                 )
 
-        def std_stage(b):
+        def rstd_stage(b):
             nh = M_BATCHES[b] * H
             st_v = st_of[b][:].rearrange("p (n t) -> p n t", t=3)
-            std = stats.tile([P, JMAX * H], F32)
+            rstd = stats.tile([P, JMAX * H], F32)
             nc.scalar.activation(
-                out=std[:, :nh], in_=st_v[:, :nh, 2], func=ACTF.Sqrt, bias=eps_t[:, 0:1], scale=1.0 / HS
+                out=rstd[:, :nh],
+                in_=st_v[:, :nh, 2],
+                func=ACTF.Abs_reciprocal_sqrt,
+                bias=eps_t[:, 0:1],
+                scale=1.0 / HS,
             )
             negmean = stats.tile([P, JMAX * H], F32)
             nc.scalar.activation(out=negmean[:, :nh], in_=st_v[:, :nh, 1], func=ACTF.Copy, scale=-1.0)
             nm_of[b] = negmean
-            std_of[b] = std
-
-        def rstd_stage(b):
-            nh = M_BATCHES[b] * H
-            rstd = stats.tile([P, JMAX * H], F32)
-            nc.vector.reciprocal(out=rstd[:, :nh], in_=std_of[b][:, :nh])
             rstd_of[b] = rstd
 
         def shift_stage(b):
@@ -373,7 +381,10 @@ def tile_full_tmix_params_pc_t_kernel(tc, y, r, k, v, g_hid, g2, r_k, ln_g, ln_b
         def collect(qb, j0):
             npair = min(2, Q_BATCHES[qb] - j0)
             o_ps = o_of[qb, j0]
-            nc.vector.tensor_copy(out=z_of[qb][2][:, j0 : j0 + npair, :], in_=o_ps[:, :npair, :])
+            if Q_BATCHES[qb] > 2:
+                nc.vector.tensor_copy(out=z_of[qb][2][:, j0 : j0 + npair, :], in_=o_ps[:, :npair, :])
+            else:
+                nc.scalar.copy(out=z_of[qb][2][:, j0 : j0 + npair, :], in_=o_ps[:, :npair, :])
 
         def store(qb):
             t0 = q_first[qb] * P
@@ -382,120 +393,173 @@ def tile_full_tmix_params_pc_t_kernel(tc, y, r, k, v, g_hid, g2, r_k, ln_g, ln_b
                 out=out_f[t0 : t0 + nb * P, :].rearrange("(j p) o -> p j o", p=P), in_=z_of[qb][2][:, :nb, :]
             )
 
-        rec_due = {-3: 0, -1: 1, 0: 2, 2: 3}
-        for b in range(4, len(M_BATCHES)):
+        rec_due = {1: 3, 2: 4}
+        for b in range(5, len(M_BATCHES)):
             rec_due[m_first[b] - 3] = b
-        shift_due = {-2: 0, -1: 1, 1: 2, 2: 3}
-        for b in range(4, len(M_BATCHES)):
-            shift_due[m_first[b] - 3] = b
-        bn_due = {-3: [0], -2: [1], -1: [2, 3], 0: [4, 5], 1: [6, 7], 2: [8, 9], 3: [10]}
-        for t in range(11, NT):
+        bn_due = {0: [3, 4], 1: [5, 6], 2: [7], 3: [8, 9], 4: [10, 11]}
+        for t in range(12, NT):
             bn_due[t - 7] = [t]
         fin_due = {q_first[b] + Q_BATCHES[b]: b for b in range(len(Q_BATCHES))}
-        y_next = 0
 
         ctx.enter_context(tc.manual_schedule())
-        for i in range(-LD, NT + 4):
-            s = i + LD
-            if 0 <= s < NT:
-                ld_rk(s)
-            while y_next < min(NT, s + min(s, 3) + 1):
-                ld_y(y_next)
-                y_next += 1
-            if 0 <= i + LD_V < NT:
-                ld_v(i + LD_V)
-            if s % JMAX == 2 and s // JMAX < NT // JMAX:
-                ld_gh(s // JMAX)
-            if s == 1:
-                nc.sync.dma_start(out=g2_sb[:], in_=g2)
-            if i == -3:
-                nc.sync.dma_start(out=w_raw[:], in_=W_o.rearrange("(a p) c -> p a c", p=P))
-            live = 0 <= i < NT
+
+        ld_y(0)
+        ld_rk(0)
+        ld_y(1)
+        ld_rk(1)
+        ld_v(0)
+        ld_gh(0)
+        nc.sync.dma_start(out=g2_sb[:], in_=g2)
+        ld_y(2)
+        ld_rk(2)
+        ld_y(3)
+        ld_y(4)
+        ld_v(1)
+        ld_rk(3)
+        ld_y(5)
+        ld_rk(4)
+        ld_y(6)
+        ld_v(2)
+        ld_y(7)
+        nc.sync.dma_start(out=w_raw[:], in_=W_o.rearrange("(a p) c -> p a c", p=P))
+        ld_rk(5)
+        ld_y(8)
+        ld_v(3)
+        ld_y(9)
+        ld_gh(1)
+
+        bn(0, 0)
+        bn(0, 1)
+        rstd_stage(0)
+        shift_stage(0)
+        prep_rk()
+        pair_rk(nc.vector, 0)
+        weigh(nc.vector, 0)
+        pair_rk(nc.gpsimd, 1)
+        dot_fold(0)
+        bn(1, 0)
+        bn(1, 1)
+        norm_rows(0)
+        dot_copy(0)
+        dot_back(0)
+        prep_ln()
+        dot_sum(0)
+        rstd_stage(1)
+        shift_stage(1)
+        weigh(nc.gpsimd, 1)
+        bonus_rows(0)
+        gh_turn(0)
+        gh_copy(0)
+        prep_g2()
+        bn(2, 0)
+        bn(2, 1)
+        rstd_stage(2)
+        shift_stage(2)
+        dot_fold(1)
+        dot_copy(1)
+        dot_back(1)
+        dot_sum(1)
+        pair_rk(nc.vector, 2)
+        weigh(nc.gpsimd, 2)
+
+        for i in range(0, NT + 4):
+            if i + 6 < NT:
+                ld_rk(i + 6)
+            if i + 10 < NT:
+                ld_y(i + 10)
+            if i + 4 < NT:
+                ld_v(i + 4)
+            if i % JMAX == 1 and i // JMAX + 2 < NT // JMAX:
+                ld_gh(i // JMAX + 2)
+            live = i < NT
             prev = 0 <= i - 1 < NT
-            nxt = 0 <= i + 1 < NT
-            fold = 0 <= i + 2 < NT
-            prod = 0 <= i + 3 < NT
+            nxt = i + 1 < NT
+            fold = i + 2 < NT
             bl = bn_due.get(i, [])
-            if i == -3:
-                pair_rk(0)
-                weigh(0)
+            early = i < 3
             if nxt:
                 norm_rows(i + 1)
             if live:
                 turn_n(i, 0)
                 turn_w(i, 0)
+            for t in bl[:1]:
+                bn(t, 0)
+                if len(bl) > 1:
+                    bn(t, 1)
             if prev:
                 gate(i - 1, 1)
             if live:
                 gate_mm(i, 0)
                 affine(i, 0)
-            for t in bl[:1]:
-                bn(t, 0)
-                if i < 4:
-                    bn(t, 1)
-            if fold:
+            if i in (1, 2):
+                proj_turn(i - 1)
+            if fold and not early:
                 dot_fold(i + 2)
-            if (i + 1) % JMAX == 0 and 0 <= i + 1 < NT:
+            if (i + 1) % JMAX == 0 and i + 1 < NT:
                 gh_turn((i + 1) // JMAX)
             if live:
                 add(i, 0)
             if i in rec_due:
-                std_stage(rec_due[i])
+                rstd_stage(rec_due[i])
             if nxt:
                 bonus_rows(i + 1)
+            last = i == NT - 1
+            if live and last:
+                turn_n(i, 1)
+                turn_w(i, 1)
             if i - 1 in fin_due:
                 project(fin_due[i - 1], 0)
             if i - 2 in fin_due and Q_BATCHES[fin_due[i - 2]] > 2:
                 project(fin_due[i - 2], 2)
-            if live:
+            if live and not last:
                 turn_n(i, 1)
                 turn_w(i, 1)
+            if live:
                 affine(i, 1)
-            if (i + 1) % JMAX == 0 and 0 <= i + 1 < NT:
+            if i in (1, 2):
+                proj_copy(i - 1)
+            if (i + 1) % JMAX == 0 and i + 1 < NT:
                 gh_copy((i + 1) // JMAX)
-            if fold:
+            if fold and not early:
                 dot_copy(i + 2)
                 dot_back(i + 2)
             if live:
                 gate_mm(i, 1)
-            if i >= 4:
-                for t in bl:
-                    bn(t, 1)
-            else:
-                for t in bl[1:]:
-                    bn(t, 0)
-                    bn(t, 1)
+            if len(bl) > 1:
+                bn(bl[1], 0)
+                bn(bl[1], 1)
+            elif bl:
+                bn(bl[0], 1)
             if live:
                 gate(i, 0)
-            if fold:
+            if fold and not early:
+                dot_sum(i + 2)
+            if fold and early:
+                dot_fold(i + 2)
+                dot_copy(i + 2)
+                dot_back(i + 2)
                 dot_sum(i + 2)
             if i in fin_due:
                 quant(fin_due[i])
-            if i >= 0 and (i + 4) % JMAX == 0 and i + 4 < NT:
-                pair_rk(i + 4)
-            if i in rec_due:
-                rstd_stage(rec_due[i])
-            if prod and i > -3 and (i + 3) % JMAX != 0:
-                pair_rk(i + 3)
-            if i in shift_due and i < 4:
-                shift_stage(shift_due[i])
-            if prod and i > -3:
-                weigh(i + 3)
-            if i in shift_due and i >= 4:
-                shift_stage(shift_due[i])
+            if i % JMAX == 0 and i + 4 < NT:
+                pair_rk(nc.vector, i + 4)
+            if i == JMAX:
+                proj_quant(0)
+                proj_quant(1)
+            if i + 3 < NT:
+                if i % JMAX != 1:
+                    pair_rk(nc.gpsimd, i + 3)
+                if early and i in rec_due:
+                    shift_stage(rec_due[i])
+                weigh(nc.gpsimd, i + 3)
+            if i in rec_due and not early:
+                shift_stage(rec_due[i])
             if i - 1 in fin_due:
                 collect(fin_due[i - 1], 0)
             if i - 2 in fin_due and Q_BATCHES[fin_due[i - 2]] > 2:
                 collect(fin_due[i - 2], 2)
             if live:
                 add(i, 1)
-            if i == -3:
-                prep_g2()
-            if i in (1, 2):
-                proj_turn(i - 1)
-                proj_copy(i - 1)
-            if i in (2, 3):
-                proj_quant(i - 2)
             if i - 2 in fin_due and Q_BATCHES[fin_due[i - 2]] <= 2:
                 store(fin_due[i - 2])
             if i - 3 in fin_due and Q_BATCHES[fin_due[i - 3]] > 2:

@@ -393,10 +393,10 @@ def tile_full_tmix_params_pc_t_kernel(tc, y, r, k, v, g_hid, g2, r_k, ln_g, ln_b
                 out=out_f[t0 : t0 + nb * P, :].rearrange("(j p) o -> p j o", p=P), in_=z_of[qb][2][:, :nb, :]
             )
 
-        rec_due = {1: 3, 2: 4}
+        rec_due = {0: 2, 1: 3, 3: 4}
         for b in range(5, len(M_BATCHES)):
             rec_due[m_first[b] - 3] = b
-        bn_due = {0: [3, 4], 1: [5, 6], 2: [7], 3: [8, 9], 4: [10, 11]}
+        bn_due = {0: [3, 4], 1: [5], 2: [6, 7], 3: [8, 9], 4: [10, 11]}
         for t in range(12, NT):
             bn_due[t - 7] = [t]
         fin_due = {q_first[b] + Q_BATCHES[b]: b for b in range(len(Q_BATCHES))}
@@ -435,32 +435,30 @@ def tile_full_tmix_params_pc_t_kernel(tc, y, r, k, v, g_hid, g2, r_k, ln_g, ln_b
         prep_rk()
         pair_rk(nc.vector, 0)
         weigh(nc.vector, 0)
-        pair_rk(nc.gpsimd, 1)
+        pair_rk(nc.vector, 1)
+        weigh(nc.gpsimd, 1)
         dot_fold(0)
-        bn(1, 0)
-        bn(1, 1)
         norm_rows(0)
         dot_copy(0)
         dot_back(0)
-        prep_ln()
+        bn(1, 0)
         dot_sum(0)
-        rstd_stage(1)
-        shift_stage(1)
-        weigh(nc.gpsimd, 1)
-        bonus_rows(0)
+        bn(1, 1)
         gh_turn(0)
         gh_copy(0)
+        bonus_rows(0)
+        rstd_stage(1)
         prep_g2()
-        bn(2, 0)
-        bn(2, 1)
-        rstd_stage(2)
-        shift_stage(2)
+        shift_stage(1)
+        pair_rk(nc.vector, 2)
+        weigh(nc.gpsimd, 2)
         dot_fold(1)
         dot_copy(1)
         dot_back(1)
+        bn(2, 0)
         dot_sum(1)
-        pair_rk(nc.vector, 2)
-        weigh(nc.gpsimd, 2)
+        bn(2, 1)
+        prep_ln()
 
         for i in range(0, NT + 4):
             if i + 6 < NT:

@@ -341,9 +341,9 @@ def tile_full_tmix_params_pc_t_kernel(tc, y, r, k, v, g_hid, g2, r_k, ln_g, ln_b
                 grp = big.tile([P, JMAX, NPASS, P, 4], BF16, align_bytes=64)
                 grp_of[qb] = grp
             nc.vector.tensor_tensor(
-                out=grp_of[qb][:, qj, g].rearrange("p (c i) u -> p c u i", i=4),
-                in0=f_of[t, g][:].rearrange("p u (c i) -> p c u i", i=4),
-                in1=gps_of[t, g][:].rearrange("p u (c i) -> p c u i", i=4),
+                out=grp_of[qb][:, qj, g].rearrange("p (c i) u -> p c u i", i=2),
+                in0=f_of[t, g][:].rearrange("p u (c i) -> p c u i", i=2),
+                in1=gps_of[t, g][:].rearrange("p u (c i) -> p c u i", i=2),
                 op=ALU.mult,
             )
 

@@ -272,8 +272,8 @@ def tile_full_tmix_params_pc_t_kernel(tc, y, r, k, v, g_hid, g2, r_k, ln_g, ln_b
                 col = mj * H + h
                 q0 = (h % 8) * 16
                 nc.scalar.activation(
-                    out=n_t[:, h // 8, :, q0 : q0 + 16],
-                    in_=y_of[t][:, h * HS : (h + 1) * HS].rearrange("p (q u) -> p u q", u=4),
+                    out=n_t[:, h // 8, :, q0 : q0 + 16].rearrange("p u (c i) -> p c u i", i=4),
+                    in_=y_of[t][:, h * HS : (h + 1) * HS].rearrange("p (c i u) -> p c u i", i=4, u=4),
                     func=ACTF.Identity,
                     bias=shift[:, col : col + 1],
                     scale=rstd[:, col : col + 1],
@@ -285,8 +285,8 @@ def tile_full_tmix_params_pc_t_kernel(tc, y, r, k, v, g_hid, g2, r_k, ln_g, ln_b
             for h in range(H):
                 q0 = (h % 8) * 16
                 nc.scalar.activation(
-                    out=w_t2[:, h // 8, :, q0 : q0 + 16],
-                    in_=v_of[t][:, h * HS : (h + 1) * HS].rearrange("p (q u) -> p u q", u=4),
+                    out=w_t2[:, h // 8, :, q0 : q0 + 16].rearrange("p u (c i) -> p c u i", i=4),
+                    in_=v_of[t][:, h * HS : (h + 1) * HS].rearrange("p (c i u) -> p c u i", i=4, u=4),
                     func=ACTF.Copy,
                     scale=dot_of[t][:, h : h + 1],
                 )

@@ -99,10 +99,7 @@ def tile_full_tmix_params_pc_t_kernel(tc, y, r, k, v, g_hid, g2, r_k, ln_g, ln_b
             gh_of[grp_i] = gh
 
         rk_row = const.tile([P, C], BF16)
-        nc.vector.memset(rk_row[:], 0.0)
-        nc.scalar.dma_start(out=rk_row[0:1, :], in_=r_k.rearrange("(o h) c -> o (h c)", o=1))
         ones_b = const.tile([P, P], BF16)
-        nc.gpsimd.memset(ones_b[:], 1.0)
         lng_raw = const.tile([P, NPASS, 4], BF16)
         nc.scalar.dma_start(out=lng_raw[:], in_=ln_g.rearrange("(g p u) -> p g u", g=NPASS, u=4))
         lnb_raw = const.tile([P, NPASS, 4], BF16)
@@ -110,16 +107,11 @@ def tile_full_tmix_params_pc_t_kernel(tc, y, r, k, v, g_hid, g2, r_k, ln_g, ln_b
         g2_sb = const.tile([P, C], BF16)
         w_raw = const.tile([P, 2, C], BF16)
 
-        ident_b = const.tile([P, P], BF16)
-        make_identity(nc, ident_b[:])
-        ident_f = const.tile([P, P], F32)
-        make_identity(nc, ident_f[:])
         zero_t = const.tile([P, 1], F32)
-        nc.gpsimd.memset(zero_t[:], 0.0)
         eps_t = const.tile([P, 1], F32)
-        nc.vector.tensor_scalar(
-            out=eps_t[:], in0=zero_t[:], scalar1=1.0, scalar2=EPS_GN, op0=ALU.mult, op1=ALU.add
-        )
+        ident_b = const.tile([P, P], BF16)
+        ident_f = const.tile([P, P], F32)
+        head_of = const.tile([P, H], F32)
         lgb = const.tile([P, 16], F32)
         rk_perm = const.tile([P, DJ, H, DI], BF16)
 
@@ -129,7 +121,8 @@ def tile_full_tmix_params_pc_t_kernel(tc, y, r, k, v, g_hid, g2, r_k, ln_g, ln_b
                 nc.tensor.matmul(
                     rk_ps[:], lhsT=ones_b[:], rhs=rk_row[:, g * 512 : (g + 1) * 512], start=True, stop=True
                 )
-                nc.scalar.copy(
+                copy = nc.scalar.copy if g == 0 else nc.vector.tensor_copy
+                copy(
                     out=rk_perm[:, :, g * 8 : (g + 1) * 8, :],
                     in_=rk_ps[:].rearrange("p (h j i) -> p j h i", j=DJ, i=DI),
                 )
@@ -204,16 +197,11 @@ def tile_full_tmix_params_pc_t_kernel(tc, y, r, k, v, g_hid, g2, r_k, ln_g, ln_b
             dsb_of[t] = d_sb
 
         def dot_back(t):
-            nc.tensor.transpose(dps_of[t][:, 1, :], dsb_of[t][:], ident_f[:])
+            nc.tensor.matmul(dps_of[t][:, 1, 0:H], lhsT=dsb_of[t][:], rhs=head_of[:], start=True, stop=True)
 
         def dot_sum(t):
             dot = stats.tile([P, H], F32)
-            nc.vector.tensor_reduce(
-                out=dot[:],
-                in_=dps_of[t][:, 1, :].rearrange("p (h i) -> p h i", i=DI),
-                axis=AX.X,
-                op=ALU.add,
-            )
+            nc.vector.tensor_copy(out=dot[:], in_=dps_of[t][:, 1, 0:H])
             dot_of[t] = dot
 
         def bn(t, half):
@@ -403,7 +391,16 @@ def tile_full_tmix_params_pc_t_kernel(tc, y, r, k, v, g_hid, g2, r_k, ln_g, ln_b
 
         ctx.enter_context(tc.manual_schedule())
 
+        nc.vector.memset(rk_row[:].bitcast(U32), 0)
+        nc.vector.memset(zero_t[:], 0.0)
+        nc.vector.tensor_scalar(
+            out=eps_t[:], in0=zero_t[:], scalar1=1.0, scalar2=EPS_GN, op0=ALU.mult, op1=ALU.add
+        )
+        nc.gpsimd.memset(ones_b[:], 1.0)
+        make_identity(nc, ident_f[:])
+        make_identity(nc, ident_b[:])
         ld_y(0)
+        nc.sync.dma_start(out=rk_row[0:1, :], in_=r_k.rearrange("(o h) c -> o (h c)", o=1))
         ld_rk(0)
         ld_y(1)
         ld_rk(1)
@@ -428,27 +425,30 @@ def tile_full_tmix_params_pc_t_kernel(tc, y, r, k, v, g_hid, g2, r_k, ln_g, ln_b
         ld_y(9)
         ld_gh(1)
 
+        nc.vector.tensor_reduce(
+            out=head_of[:], in_=ident_f[:].rearrange("p (h i) -> p h i", i=DI), axis=AX.X, op=ALU.add
+        )
         bn(0, 0)
         bn(0, 1)
         rstd_stage(0)
         shift_stage(0)
-        prep_rk()
         pair_rk(nc.vector, 0)
+        prep_rk()
         weigh(nc.vector, 0)
         pair_rk(nc.vector, 1)
         weigh(nc.gpsimd, 1)
         dot_fold(0)
+        gh_turn(0)
         norm_rows(0)
+        gh_copy(0)
+        prep_g2()
         dot_copy(0)
         dot_back(0)
         bn(1, 0)
         dot_sum(0)
         bn(1, 1)
-        gh_turn(0)
-        gh_copy(0)
         bonus_rows(0)
         rstd_stage(1)
-        prep_g2()
         shift_stage(1)
         pair_rk(nc.vector, 2)
         weigh(nc.gpsimd, 2)
@@ -501,17 +501,13 @@ def tile_full_tmix_params_pc_t_kernel(tc, y, r, k, v, g_hid, g2, r_k, ln_g, ln_b
                 rstd_stage(rec_due[i])
             if nxt:
                 bonus_rows(i + 1)
-            last = i == NT - 1
-            if live and last:
+            if live:
                 turn_n(i, 1)
                 turn_w(i, 1)
             if i - 1 in fin_due:
                 project(fin_due[i - 1], 0)
             if i - 2 in fin_due and Q_BATCHES[fin_due[i - 2]] > 2:
                 project(fin_due[i - 2], 2)
-            if live and not last:
-                turn_n(i, 1)
-                turn_w(i, 1)
             if live:
                 affine(i, 1)
             if i in (1, 2):

from contextlib import ExitStack

import concourse.mybir as mybir
from concourse.masks import make_identity

F32 = mybir.dt.float32
BF16 = mybir.dt.bfloat16
U32 = mybir.dt.uint32
U8 = mybir.dt.uint8
FP8X4 = mybir.dt.float8_e4m3fn_x4
ALU = mybir.AluOpType
ACTF = mybir.ActivationFunctionType
AX = mybir.AxisListType

P = 128
TOK = 4096
NT = TOK // P
C = 1024
CO = 256
HS = 64
H = C // HS
DG = 128
EPS_GN = 0.00064
NPASS = C // 512
JMAX = 4
DI = 8
DJ = C // P
M_BATCHES = (1, 1, 1, 2, 2) + (4,) * 6 + (1,)
Q_BATCHES = (4,) * 7 + (2, 1, 1)
LD = 9
LD_Y = LD + 2
LD_V = 7

FLOPS = 2 * TOK * DG * C + 2 * TOK * C * CO


def batch_maps(sizes):
    first = []
    where = {}
    t = 0
    for b, n in enumerate(sizes):
        first.append(t)
        for j in range(n):
            where[t + j] = (b, j)
        t += n
    return first, where


def tile_full_tmix_params_pc_t_kernel(tc, y, r, k, v, g_hid, g2, r_k, ln_g, ln_b, W_o, out):
    nc = tc.nc
    y_f = y.flatten_outer_dims()
    r_f = r.flatten_outer_dims()
    k_f = k.flatten_outer_dims()
    v_f = v.flatten_outer_dims()
    gh_f = g_hid.flatten_outer_dims()
    out_f = out.flatten_outer_dims()
    m_first, m_where = batch_maps(M_BATCHES)
    q_first, q_where = batch_maps(Q_BATCHES)

    with ExitStack() as ctx:
        const = ctx.enter_context(tc.tile_pool(name="const", bufs=1))
        ypool = ctx.enter_context(tc.tile_pool(name="ypool", bufs=LD_Y + 1))
        rkpool = ctx.enter_context(tc.tile_pool(name="rkpool", bufs=LD - 2))
        vpool = ctx.enter_context(tc.tile_pool(name="vpool", bufs=LD_V + 1))
        work = ctx.enter_context(tc.tile_pool(name="work", bufs=3))
        big = ctx.enter_context(tc.tile_pool(name="big", bufs=2))
        stats = ctx.enter_context(tc.tile_pool(name="stats", bufs=5))
        small = ctx.enter_context(tc.tile_pool(name="small", bufs=3))
        psum = ctx.enter_context(tc.psum_pool(name="psum", bufs=2))

        y_of, r_of, k_of, v_of, gh_of, ght_of, q_of, dot_of = {}, {}, {}, {}, {}, {}, {}, {}
        st_of, nm_of, rstd_of, shift_of, grp_of, z_of, wg_of, o_of = {}, {}, {}, {}, {}, {}, {}, {}
        nt_of, wt_of, nps_of, wps_of, gps_of, e_of, f_of, dps_of, dsb_of = {}, {}, {}, {}, {}, {}, {}, {}, {}

        def ld_y(t):
            y_t = ypool.tile([P, C], BF16)
            nc.sync.dma_start(out=y_t[:], in_=y_f[t * P : (t + 1) * P, :])
            y_of[t] = y_t

        def ld_rk(t):
            r_t = rkpool.tile([P, C], BF16)
            nc.sync.dma_start(out=r_t[:], in_=r_f[t * P : (t + 1) * P, :])
            r_of[t] = r_t
            k_t = rkpool.tile([P, C], BF16)
            nc.sync.dma_start(out=k_t[:], in_=k_f[t * P : (t + 1) * P, :])
            k_of[t] = k_t

        def ld_v(t):
            v_t = vpool.tile([P, C], BF16)
            nc.sync.dma_start(out=v_t[:], in_=v_f[t * P : (t + 1) * P, :])
            v_of[t] = v_t

        def ld_gh(grp_i):
            gh = small.tile([P, JMAX, DG], BF16)
            nc.sync.dma_start(
                out=gh[:],
                in_=gh_f[grp_i * JMAX * P : (grp_i + 1) * JMAX * P, :].rearrange("(j p) d -> p j d", p=P),
            )
            gh_of[grp_i] = gh

        rk_row = const.tile([P, C], BF16)
        ones_b = const.tile([P, P], BF16)
        lng_raw = const.tile([P, NPASS, 4], BF16)
        nc.scalar.dma_start(out=lng_raw[:], in_=ln_g.rearrange("(g p u) -> p g u", g=NPASS, u=4))
        lnb_raw = const.tile([P, NPASS, 4], BF16)
        nc.scalar.dma_start(out=lnb_raw[:], in_=ln_b.rearrange("(g p u) -> p g u", g=NPASS, u=4))
        g2_sb = const.tile([P, C], BF16)
        w_raw = const.tile([P, 2, C], BF16)

        zero_t = const.tile([P, 1], F32)
        eps_t = const.tile([P, 1], F32)
        ident_b = const.tile([P, P], BF16)
        ident_f = const.tile([P, P], F32)
        head_of = const.tile([P, H], F32)
        lgb = const.tile([P, 16], F32)
        rk_perm = const.tile([P, DJ, H, DI], BF16)

        def prep_rk():
            for g in range(NPASS):
                rk_ps = psum.tile([P, 512], F32, tag=("misc", "dot")[g], bufs=1)
                nc.tensor.matmul(
                    rk_ps[:], lhsT=ones_b[:], rhs=rk_row[:, g * 512 : (g + 1) * 512], start=True, stop=True
                )
                copy = nc.scalar.copy if g == 0 else nc.vector.tensor_copy
                copy(
                    out=rk_perm[:, :, g * 8 : (g + 1) * 8, :],
                    in_=rk_ps[:].rearrange("p (h j i) -> p j h i", j=DJ, i=DI),
                )

        def prep_ln():
            nc.vector.tensor_copy(out=lgb[:, 0:8], in_=lng_raw[:].rearrange("p g u -> p (g u)"))
            nc.vector.tensor_copy(out=lgb[:, 8:16], in_=lnb_raw[:].rearrange("p g u -> p (g u)"))
        g2_perm = const.tile([P, C], BF16)
        w_codes = const.tile([P, NPASS * CO], U32, align_bytes=64)
        w_scales = const.tile([P, NPASS * CO], U8, align_bytes=64)

        def prep_g2():
            nc.scalar.copy(
                out=g2_perm[:].rearrange("k (g u p) -> k g u p", g=NPASS, u=4),
                in_=g2_sb[:].rearrange("k (g p u) -> k g u p", g=NPASS, u=4),
            )

        def proj_turn(g):
            w_t = psum.tile([P, 4, CO], BF16, tag="misc", bufs=1)
            for t in range(4):
                for a in range(2):
                    nc.tensor.transpose(
                        w_t[:, t, a * P : (a + 1) * P],
                        w_raw[:, a, g * 512 + t : (g + 1) * 512 : 4],
                        ident_b[:],
                    )
            wg_of[g] = w_t

        def proj_copy(g):
            w_grp = const.tile([P, CO, 4], BF16, align_bytes=64, bufs=2)
            nc.scalar.copy(out=w_grp[:], in_=wg_of[g][:].rearrange("p t o -> p o t"))
            wg_of[g] = w_grp

        def proj_quant(g):
            nc.vector.quantize_mx(
                out=w_codes[:, g * CO : (g + 1) * CO].bitcast(FP8X4),
                scales=w_scales[:, g * CO : (g + 1) * CO],
                in_=wg_of[g][:].rearrange("p o t -> p (o t)"),
            )

        def pair_rk(eng, t):
            p_t = work.tile([P, C], F32, bufs=3)
            eng.tensor_tensor(out=p_t[:], in0=r_of[t][:], in1=k_of[t][:], op=ALU.mult)
            q_of[t] = p_t

        def weigh(eng, t):
            q = work.tile([P, DJ, H, DI], F32, bufs=4)
            eng.tensor_tensor(
                out=q[:],
                in0=q_of[t][:].rearrange("p (h j i) -> p j h i", j=DJ, i=DI),
                in1=rk_perm[:],
                op=ALU.mult,
            )
            q_of[t] = q

        def dot_fold(t):
            d_ps = psum.tile([P, 2, P], F32, tag="dot", bufs=1)
            for j in range(DJ):
                nc.tensor.matmul(
                    d_ps[:, 0, :],
                    lhsT=q_of[t][:, j].rearrange("p h i -> p (h i)"),
                    rhs=ident_f[:],
                    is_transpose=True,
                    start=(j == 0),
                    stop=(j == DJ - 1),
                )
            dps_of[t] = d_ps

        def dot_copy(t):
            d_sb = small.tile([P, P], F32)
            nc.vector.tensor_copy(out=d_sb[:], in_=dps_of[t][:, 0, :])
            dsb_of[t] = d_sb

        def dot_back(t):
            nc.tensor.matmul(dps_of[t][:, 1, 0:H], lhsT=dsb_of[t][:], rhs=head_of[:], start=True, stop=True)

        def dot_sum(t):
            dot = stats.tile([P, H], F32)
            nc.vector.tensor_copy(out=dot[:], in_=dps_of[t][:, 1, 0:H])
            dot_of[t] = dot

        def bn(t, half):
            b, j = m_where[t]
            if j == 0 and half == 0:
                st = stats.tile([P, JMAX * H * 3], F32)
                st_of[b] = st
            st = st_of[b]
            for hp in range(half * 4, half * 4 + 4):
                i0 = (j * (H // 2) + hp) * 6
                nc.vector.bn_stats(
                    out=st[:, i0 : i0 + 6],
                    in_=y_of[t][:, hp * 2 * HS : (hp + 1) * 2 * HS].rearrange("p (h c) -> p c h", h=2),
                )

        def rstd_stage(b):
            nh = M_BATCHES[b] * H
            st_v = st_of[b][:].rearrange("p (n t) -> p n t", t=3)
            rstd = stats.tile([P, JMAX * H], F32)
            nc.scalar.activation(
                out=rstd[:, :nh],
                in_=st_v[:, :nh, 2],
                func=ACTF.Abs_reciprocal_sqrt,
                bias=eps_t[:, 0:1],
                scale=1.0 / HS,
            )
            negmean = stats.tile([P, JMAX * H], F32)
            nc.scalar.activation(out=negmean[:, :nh], in_=st_v[:, :nh, 1], func=ACTF.Copy, scale=-1.0)
            nm_of[b] = negmean
            rstd_of[b] = rstd

        def shift_stage(b):
            nh = M_BATCHES[b] * H
            shift = stats.tile([P, JMAX * H], F32)
            nc.gpsimd.tensor_tensor(
                out=shift[:, :nh], in0=nm_of[b][:, :nh], in1=rstd_of[b][:, :nh], op=ALU.mult
            )
            shift_of[b] = shift

        def gh_turn(grp_i):
            gh_ps = psum.tile([P, JMAX, P], BF16, tag="misc", bufs=1)
            for j in range(JMAX):
                nc.tensor.transpose(gh_ps[:, j, :], gh_of[grp_i][:, j, :], ident_b[:])
            ght_of[grp_i] = gh_ps

        def gh_copy(grp_i):
            gh_t = small.tile([P, JMAX, P], BF16)
            nc.scalar.copy(out=gh_t[:], in_=ght_of[grp_i][:])
            ght_of[grp_i] = gh_t

        def norm_rows(t):
            mb, mj = m_where[t]
            rstd, shift = rstd_of[mb], shift_of[mb]
            n_t = work.tile([P, NPASS, 4, P], F32)
            for h in range(H):
                col = mj * H + h
                q0 = (h % 8) * 16
                nc.scalar.activation(
                    out=n_t[:, h // 8, :, q0 : q0 + 16].rearrange("p u (c i) -> p c u i", i=4),
                    in_=y_of[t][:, h * HS : (h + 1) * HS].rearrange("p (c i u) -> p c u i", i=4, u=4),
                    func=ACTF.Identity,
                    bias=shift[:, col : col + 1],
                    scale=rstd[:, col : col + 1],
                )
            nt_of[t] = n_t

        def bonus_rows(t):
            w_t2 = work.tile([P, NPASS, 4, P], F32)
            for h in range(H):
                q0 = (h % 8) * 16
                nc.scalar.activation(
                    out=w_t2[:, h // 8, :, q0 : q0 + 16].rearrange("p u (c i) -> p c u i", i=4),
                    in_=v_of[t][:, h * HS : (h + 1) * HS].rearrange("p (c i u) -> p c u i", i=4, u=4),
                    func=ACTF.Copy,
                    scale=dot_of[t][:, h : h + 1],
                )
            wt_of[t] = w_t2

        def turn_n(t, g):
            n_ps = psum.tile([P, 4, P], F32)
            for u in range(4):
                nc.tensor.transpose(n_ps[:, u, :], nt_of[t][:, g, u, :], ident_f[:])
            nps_of[t, g] = n_ps

        def turn_w(t, g):
            w_ps = psum.tile([P, 4, P], F32)
            for u in range(4):
                nc.tensor.transpose(w_ps[:, u, :], wt_of[t][:, g, u, :], ident_f[:])
            wps_of[t, g] = w_ps

        def gate_mm(t, g):
            g_ps = psum.tile([P, 4, P], F32)
            for u in range(4):
                cb = g * 4 + u
                nc.tensor.matmul(
                    g_ps[:, u, :],
                    lhsT=g2_perm[:, cb * P : (cb + 1) * P],
                    rhs=ght_of[t // JMAX][:, t % JMAX, :],
                    start=True,
                    stop=True,
                )
            gps_of[t, g] = g_ps

        def affine(t, g):
            e_t = work.tile([P, 4, P], F32)
            for u in range(4):
                cb = g * 4 + u
                nc.scalar.activation(
                    out=e_t[:, u, :],
                    in_=nps_of[t, g][:, u, :],
                    func=ACTF.Identity,
                    bias=lgb[:, 8 + cb : 9 + cb],
                    scale=lgb[:, cb : cb + 1],
                )
            e_of[t, g] = e_t

        def add(t, g):
            f_t = work.tile([P, 4, P], F32)
            nc.vector.tensor_tensor(out=f_t[:], in0=e_of[t, g][:], in1=wps_of[t, g][:], op=ALU.add)
            f_of[t, g] = f_t

        def gate(t, g):
            qb, qj = q_where[t]
            if qj == 0 and g == 0:
                grp = big.tile([P, JMAX, NPASS, P, 4], BF16, align_bytes=64)
                grp_of[qb] = grp
            nc.vector.tensor_tensor(
                out=grp_of[qb][:, qj, g].rearrange("p (c i) u -> p c u i", i=2),
                in0=f_of[t, g][:].rearrange("p u (c i) -> p c u i", i=2),
                in1=gps_of[t, g][:].rearrange("p u (c i) -> p c u i", i=2),
                op=ALU.mult,
            )

        def quant(qb):
            nb = Q_BATCHES[qb]
            z_codes = big.tile([P, JMAX * NPASS * P], U32, align_bytes=64)
            z_scales = big.tile([P, JMAX * NPASS * P], U8, align_bytes=64)
            nw = nb * NPASS * P
            nc.vector.quantize_mx(
                out=z_codes[:, :nw].bitcast(FP8X4),
                scales=z_scales[:, :nw],
                in_=grp_of[qb][:, :nb].rearrange("p j g m u -> p (j g m u)"),
            )
            o_sb = big.tile([P, JMAX, CO], F32)
            z_of[qb] = (z_codes, z_scales, o_sb)

        def project(qb, j0):
            z_codes, z_scales, o_sb = z_of[qb]
            npair = min(2, Q_BATCHES[qb] - j0)
            o_ps = psum.tile([P, 2, CO], F32, tag="misc", bufs=1)
            for u in range(npair):
                for g in range(NPASS):
                    i0 = ((j0 + u) * NPASS + g) * P
                    nc.tensor.matmul_mx(
                        out=o_ps[:, u, :],
                        lhsT=z_codes[:, i0 : i0 + P].bitcast(FP8X4),
                        lhsT_scale=z_scales[:, i0 : i0 + P],
                        rhs=w_codes[:, g * CO : (g + 1) * CO].bitcast(FP8X4),
                        rhs_scale=w_scales[:, g * CO : (g + 1) * CO],
                        start=(g == 0),
                        stop=(g == NPASS - 1),
                    )
            o_of[qb, j0] = o_ps

        def collect(qb, j0):
            npair = min(2, Q_BATCHES[qb] - j0)
            o_ps = o_of[qb, j0]
            if Q_BATCHES[qb] > 2:
                nc.vector.tensor_copy(out=z_of[qb][2][:, j0 : j0 + npair, :], in_=o_ps[:, :npair, :])
            else:
                nc.scalar.copy(out=z_of[qb][2][:, j0 : j0 + npair, :], in_=o_ps[:, :npair, :])

        def store(qb):
            t0 = q_first[qb] * P
            nb = Q_BATCHES[qb]
            nc.sync.dma_start(
                out=out_f[t0 : t0 + nb * P, :].rearrange("(j p) o -> p j o", p=P), in_=z_of[qb][2][:, :nb, :]
            )

        rec_due = {0: 2, 1: 3, 3: 4}
        for b in range(5, len(M_BATCHES)):
            rec_due[m_first[b] - 3] = b
        bn_due = {0: [3, 4], 1: [5], 2: [6, 7], 3: [8, 9], 4: [10, 11]}
        for t in range(12, NT):
            bn_due[t - 7] = [t]
        fin_due = {q_first[b] + Q_BATCHES[b]: b for b in range(len(Q_BATCHES))}

        ctx.enter_context(tc.manual_schedule())

        nc.vector.memset(rk_row[:].bitcast(U32), 0)
        nc.vector.memset(zero_t[:], 0.0)
        nc.vector.tensor_scalar(
            out=eps_t[:], in0=zero_t[:], scalar1=1.0, scalar2=EPS_GN, op0=ALU.mult, op1=ALU.add
        )
        nc.gpsimd.memset(ones_b[:], 1.0)
        make_identity(nc, ident_f[:])
        make_identity(nc, ident_b[:])
        ld_y(0)
        nc.sync.dma_start(out=rk_row[0:1, :], in_=r_k.rearrange("(o h) c -> o (h c)", o=1))
        ld_rk(0)
        ld_y(1)
        ld_rk(1)
        ld_v(0)
        ld_gh(0)
        nc.sync.dma_start(out=g2_sb[:], in_=g2)
        ld_y(2)
        ld_rk(2)
        ld_y(3)
        ld_y(4)
        ld_v(1)
        ld_rk(3)
        ld_y(5)
        ld_rk(4)
        ld_y(6)
        ld_v(2)
        ld_y(7)
        nc.sync.dma_start(out=w_raw[:], in_=W_o.rearrange("(a p) c -> p a c", p=P))
        ld_rk(5)
        ld_y(8)
        ld_v(3)
        ld_y(9)
        ld_gh(1)

        nc.vector.tensor_reduce(
            out=head_of[:], in_=ident_f[:].rearrange("p (h i) -> p h i", i=DI), axis=AX.X, op=ALU.add
        )
        bn(0, 0)
        bn(0, 1)
        rstd_stage(0)
        shift_stage(0)
        pair_rk(nc.vector, 0)
        prep_rk()
        weigh(nc.vector, 0)
        pair_rk(nc.vector, 1)
        weigh(nc.gpsimd, 1)
        dot_fold(0)
        gh_turn(0)
        norm_rows(0)
        gh_copy(0)
        prep_g2()
        dot_copy(0)
        dot_back(0)
        bn(1, 0)
        dot_sum(0)
        bn(1, 1)
        bonus_rows(0)
        rstd_stage(1)
        shift_stage(1)
        pair_rk(nc.vector, 2)
        weigh(nc.gpsimd, 2)
        dot_fold(1)
        dot_copy(1)
        dot_back(1)
        bn(2, 0)
        dot_sum(1)
        bn(2, 1)
        prep_ln()

        for i in range(0, NT + 4):
            if i + 6 < NT:
                ld_rk(i + 6)
            if i + 10 < NT:
                ld_y(i + 10)
            if i + 4 < NT:
                ld_v(i + 4)
            if i % JMAX == 1 and i // JMAX + 2 < NT // JMAX:
                ld_gh(i // JMAX + 2)
            live = i < NT
            prev = 0 <= i - 1 < NT
            nxt = i + 1 < NT
            fold = i + 2 < NT
            bl = bn_due.get(i, [])
            early = i < 3
            if nxt:
                norm_rows(i + 1)
            if live:
                turn_n(i, 0)
                turn_w(i, 0)
            for t in bl[:1]:
                bn(t, 0)
                if len(bl) > 1:
                    bn(t, 1)
            if prev:
                gate(i - 1, 1)
            if live:
                gate_mm(i, 0)
                affine(i, 0)
            if i in (1, 2):
                proj_turn(i - 1)
            if fold and not early:
                dot_fold(i + 2)
            if (i + 1) % JMAX == 0 and i + 1 < NT:
                gh_turn((i + 1) // JMAX)
            if live:
                add(i, 0)
            if i in rec_due:
                rstd_stage(rec_due[i])
            if nxt:
                bonus_rows(i + 1)
            if live:
                turn_n(i, 1)
                turn_w(i, 1)
            if i - 1 in fin_due:
                project(fin_due[i - 1], 0)
            if i - 2 in fin_due and Q_BATCHES[fin_due[i - 2]] > 2:
                project(fin_due[i - 2], 2)
            if live:
                affine(i, 1)
            if i in (1, 2):
                proj_copy(i - 1)
            if (i + 1) % JMAX == 0 and i + 1 < NT:
                gh_copy((i + 1) // JMAX)
            if fold and not early:
                dot_copy(i + 2)
                dot_back(i + 2)
            if live:
                gate_mm(i, 1)
            if len(bl) > 1:
                bn(bl[1], 0)
                bn(bl[1], 1)
            elif bl:
                bn(bl[0], 1)
            if live:
                gate(i, 0)
            if fold and not early:
                dot_sum(i + 2)
            if fold and early:
                dot_fold(i + 2)
                dot_copy(i + 2)
                dot_back(i + 2)
                dot_sum(i + 2)
            if i in fin_due:
                quant(fin_due[i])
            if i % JMAX == 0 and i + 4 < NT:
                pair_rk(nc.vector, i + 4)
            if i == JMAX:
                proj_quant(0)
                proj_quant(1)
            if i + 3 < NT:
                if i % JMAX != 1:
                    pair_rk(nc.gpsimd, i + 3)
                if early and i in rec_due:
                    shift_stage(rec_due[i])
                weigh(nc.gpsimd, i + 3)
            if i in rec_due and not early:
                shift_stage(rec_due[i])
            if i - 1 in fin_due:
                collect(fin_due[i - 1], 0)
            if i - 2 in fin_due and Q_BATCHES[fin_due[i - 2]] > 2:
                collect(fin_due[i - 2], 2)
            if live:
                add(i, 1)
            if i - 2 in fin_due and Q_BATCHES[fin_due[i - 2]] <= 2:
                store(fin_due[i - 2])
            if i - 3 in fin_due and Q_BATCHES[fin_due[i - 3]] > 2:
                store(fin_due[i - 3])
